import numpy as np
import ml_dtypes


def mxq(x, axis, fmt="e4m3"):
    dtype, down = {"e4m3": (ml_dtypes.float8_e4m3fn, 7), "e5m2": (ml_dtypes.float8_e5m2, 14)}[fmt]
    v = np.moveaxis(np.asarray(x, np.float32).astype(ml_dtypes.bfloat16).astype(np.float64), axis, -1)
    blocks = v.reshape(v.shape[:-1] + (-1, 32))
    amax = np.abs(blocks).max(-1, keepdims=True)
    byte = np.maximum(np.where(amax > 0, np.frexp(amax)[1] - 1 + 127, 0) - down, 1)
    scale = np.exp2(byte - 127.0)
    codes = (blocks / scale).astype(np.float32).astype(dtype).astype(np.float64)
    return np.moveaxis((codes * scale).reshape(v.shape), -1, axis)


WIDE = False


def mx_kscale(k):
    if not WIDE:
        return np.ones(k)
    levels = np.array([10, -10, 5, -5, 0])
    a = np.random.permutation(np.resize(levels, k // 512 * 4)).reshape(k // 512, 4)
    idx = np.arange(k)
    return np.exp2(a[idx // 512, idx % 128 // 32])


BF16 = ml_dtypes.bfloat16


def bf(x):
    return np.asarray(x, np.float32).astype(BF16)


def f64(x):
    return np.asarray(x).astype(np.float64)


B, F, L, SEG, PRED, D, H = 4, 128, 48, 24, 192, 1024, 1024
R = B * F
EPS = 1e-15
MAXN = 1.0 - 1e-5


def norm(a):
    return np.sqrt(np.maximum(np.sum(a * a, axis=-1, keepdims=True), EPS))


def artanh(r):
    c = np.clip(r, -1.0 + 1e-7, 1.0 - 1e-7)
    return 0.5 * np.log((1.0 + c) / (1.0 - c))


def projx(a):
    n = norm(a)
    return np.where(n > MAXN, a * (MAXN / n), a)


def expmap0(v):
    n = norm(v)
    return np.tanh(n) * v / n


def mobius_add(x, y):
    x2 = np.sum(x * x, -1, keepdims=True)
    y2 = np.sum(y * y, -1, keepdims=True)
    xy = np.sum(x * y, -1, keepdims=True)
    num = (1.0 + 2.0 * xy + y2) * x + (1.0 - x2) * y
    den = 1.0 + 2.0 * xy + x2 * y2
    return num / np.maximum(den, EPS)


def setup_inputs():
    s = mx_kscale(D)
    c = np.exp2(np.ceil(np.log2(np.sqrt(np.mean(s * s)))))
    return {"v_init": bf(np.random.standard_normal((R, D)) * 0.55 / np.sqrt(D) * s / c),
            "W_vel": bf(np.random.standard_normal((D, D)) * 1.5 / np.sqrt(D) * c / s[None, :]),
            "b_vel": bf(np.random.standard_normal(D) * 0.4 / np.sqrt(D))}


def reference(v_init, W_vel, b_vel):
    x = f64(v_init)
    mx = mxq(x, 1, "e4m3") @ mxq(f64(W_vel), 1, "e4m3").T
    xn = norm(x)
    mxn = norm(mx)
    p = np.tanh(mxn / xn * artanh(xn)) * mx / mxn
    return projx(mobius_add(p, expmap0(f64(b_vel))))

@@ -1,0 +1,279 @@
+from contextlib import ExitStack
+
+import concourse.mybir as mybir
+from concourse.masks import make_identity
+
+F32 = mybir.dt.float32
+BF16 = mybir.dt.bfloat16
+U32 = mybir.dt.uint32
+U8 = mybir.dt.uint8
+I32 = mybir.dt.int32
+FP8X4 = mybir.dt.float8_e4m3fn_x4
+ALU = mybir.AluOpType
+ACT = mybir.ActivationFunctionType
+
+P = 128
+ROWS = 512
+K = 1024
+N = 1024
+K_PASS = 4 * P
+PASSES = K // K_PASS
+PAIR = 2 * P
+ROW_TILES = ROWS // P
+BANK = 512
+HALVES = N // BANK
+WORDS = K // 2
+
+EPS = 1e-15
+MAXN = 1.0 - 1e-5
+FLOPS = 2 * ROWS * K * N
+
+
+def transpose_and_quantise(nc, psum, stage, bank_tag, pair_words, g, ident, codes, scales):
+    flipped = psum.tile([P, 2, PAIR], F32, tag=bank_tag, name="flipped")
+    for u in range(2):
+        for a in range(2):
+            first = WORDS * a + 2 * P * g + P * u
+            nc.tensor.transpose(
+                flipped[:, u, P * a : P * (a + 1)], pair_words[:, first : first + P], ident[:]
+            )
+    grouped = stage.tile([P, 4 * PAIR], BF16, align_bytes=64, name="grouped")
+    nc.scalar.copy(
+        out=grouped[:].bitcast(F32).rearrange("p (c u) -> p c u", u=2),
+        in_=flipped[:].rearrange("p u c -> p c u"),
+    )
+    nc.vector.quantize_mx(out=codes.bitcast(FP8X4), scales=scales, in_=grouped[:])
+
+
+def tile_directnodecomphyperbolicforecaster_pa_kernel(tc, v_init, W_vel, b_vel, out):
+    nc = tc.nc
+    with ExitStack() as ctx:
+        keep = ctx.enter_context(tc.tile_pool(name="keep", bufs=1))
+        stage = ctx.enter_context(tc.tile_pool(name="stage", bufs=4))
+        junk = ctx.enter_context(tc.tile_pool(name="junk", bufs=2))
+        small = ctx.enter_context(tc.tile_pool(name="small", bufs=ROW_TILES))
+        rows_out = ctx.enter_context(tc.tile_pool(name="rows_out", bufs=ROW_TILES))
+        psum = ctx.enter_context(tc.psum_pool(name="psum", bufs=1))
+
+        b_row0 = keep.tile([P, N], BF16, name="b_row0")
+        nc.vector.memset(b_row0[:].bitcast(I32), 0)
+        nc.sync.dma_start(out=b_row0[0:1, :], in_=b_vel.rearrange("(o n) -> o n", o=1))
+
+        x_pairs = []
+        for xp in range(ROWS // PAIR):
+            x_pair = keep.tile([P, 2 * K], BF16, name="x_pair%d" % xp)
+            nc.sync.dma_start(
+                out=x_pair[:].rearrange("p (a k) -> p a k", a=2),
+                in_=v_init[PAIR * xp : PAIR * (xp + 1), :].rearrange("(p a) k -> p a k", a=2),
+            )
+            x_pairs.append(x_pair)
+        w_pairs = []
+        for wp in range(N // PAIR):
+            w_pair = keep.tile([P, 2 * K], BF16, name="w_pair%d" % wp)
+            nc.sync.dma_start(
+                out=w_pair[:].rearrange("p (a k) -> p a k", a=2),
+                in_=W_vel[PAIR * wp : PAIR * (wp + 1), :].rearrange("(a p) k -> p a k", p=P),
+            )
+            w_pairs.append(w_pair)
+
+        ident = keep.tile([P, P], F32, name="ident")
+        make_identity(nc, ident[:])
+        ones = keep.tile([P, P], BF16, name="ones")
+        nc.vector.memset(ones[:], 1.0)
+        exp_pair = keep.tile([P, 2], F32, name="exp_pair")
+        nc.vector.memset(exp_pair[:, 0:1], 0.5)
+        nc.vector.memset(exp_pair[:, 1:2], -0.5)
+        exp_half = keep.tile([P, ROW_TILES], F32, name="exp_half")
+        nc.vector.memset(exp_half[:], 0.5)
+        exp_neg_half = keep.tile([P, ROW_TILES], F32, name="exp_neg_half")
+        nc.vector.memset(exp_neg_half[:], -0.5)
+
+        b_psum = psum.tile([P, N], BF16, tag="bank7", name="b_psum")
+        for h in range(HALVES):
+            cols = slice(BANK * h, BANK * (h + 1))
+            nc.tensor.matmul(b_psum[:, cols], lhsT=ones[:], rhs=b_row0[:, cols], start=True, stop=True)
+        b_sq = junk.tile([P, N], BF16, name="b_sq")
+        b_sum = keep.tile([P, 1], F32, name="b_sum")
+        nc.scalar.activation(out=b_sq[:], in_=b_psum[:], func=ACT.Square, accum_out=b_sum[:])
+        b_all = keep.tile([P, N], BF16, name="b_all")
+        nc.scalar.copy(out=b_all[:], in_=b_psum[:])
+
+        x_codes = keep.tile([P, PASSES, ROWS], U32, align_bytes=64, name="x_codes")
+        x_scales = keep.tile([P, PASSES, ROWS], U8, align_bytes=64, name="x_scales")
+        x_sum = keep.tile([P, ROW_TILES], F32, name="x_sum")
+        for xp in range(ROWS // PAIR):
+            cols = slice(PAIR * xp, PAIR * (xp + 1))
+            for g in range(PASSES):
+                transpose_and_quantise(
+                    nc, psum, stage, "bank%d" % (PASSES * xp + g), x_pairs[xp][:].bitcast(F32), g,
+                    ident, x_codes[:, g, cols], x_scales[:, g, cols],
+                )
+            for a in range(2):
+                x_sq = junk.tile([P, K], F32, name="x_sq")
+                x_rows = x_pairs[xp][:, K * a : K * (a + 1)]
+                nc.vector.scalar_tensor_tensor(
+                    out=x_sq[:], in0=x_rows, scalar=1.0, in1=x_rows, op0=ALU.mult, op1=ALU.mult,
+                    accum_out=x_sum[:, 2 * xp + a : 2 * xp + a + 1],
+                )
+
+        x_sum_c = keep.tile([P, ROW_TILES], F32, name="x_sum_c")
+        nc.vector.tensor_scalar_max(out=x_sum_c[:], in0=x_sum[:], scalar1=EPS)
+        xn = keep.tile([P, ROW_TILES], F32, name="xn")
+        nc.gpsimd.tensor_tensor(out=xn[:], in0=x_sum_c[:], in1=exp_half[:], op=ALU.pow)
+        xn_inv = keep.tile([P, ROW_TILES], F32, name="xn_inv")
+        nc.gpsimd.tensor_tensor(out=xn_inv[:], in0=x_sum_c[:], in1=exp_neg_half[:], op=ALU.pow)
+        clipped = keep.tile([P, ROW_TILES], F32, name="clipped")
+        nc.vector.tensor_scalar_min(out=clipped[:], in0=xn[:], scalar1=1.0 - 1e-7)
+        one_minus = keep.tile([P, ROW_TILES], F32, name="one_minus")
+        nc.vector.tensor_scalar(
+            out=one_minus[:], in0=clipped[:], scalar1=-1.0, scalar2=1.0, op0=ALU.mult, op1=ALU.add
+        )
+        one_minus_inv = keep.tile([P, ROW_TILES], F32, name="one_minus_inv")
+        nc.vector.reciprocal(out=one_minus_inv[:], in_=one_minus[:])
+        ratio = keep.tile([P, ROW_TILES], F32, name="ratio")
+        nc.vector.scalar_tensor_tensor(
+            out=ratio[:], in0=clipped[:], scalar=1.0, in1=one_minus_inv[:], op0=ALU.add, op1=ALU.mult
+        )
+        log_ratio = keep.tile([P, ROW_TILES], F32, name="log_ratio")
+        nc.scalar.activation(out=log_ratio[:], in_=ratio[:], func=ACT.Ln)
+        gain = keep.tile([P, ROW_TILES], F32, name="gain")
+        nc.vector.scalar_tensor_tensor(
+            out=gain[:], in0=log_ratio[:], scalar=0.5, in1=xn_inv[:], op0=ALU.mult, op1=ALU.mult
+        )
+
+        b_sum_c = keep.tile([P, 1], F32, name="b_sum_c")
+        nc.vector.tensor_scalar_max(out=b_sum_c[:], in0=b_sum[:], scalar1=EPS)
+        b_roots = keep.tile([P, 2], F32, name="b_roots")
+        nc.gpsimd.tensor_tensor(
+            out=b_roots[:], in0=b_sum_c[:, 0:1].to_broadcast([P, 2]), in1=exp_pair[:], op=ALU.pow
+        )
+        b_tanh = keep.tile([P, 1], F32, name="b_tanh")
+        nc.scalar.activation(out=b_tanh[:], in_=b_roots[:, 0:1], func=ACT.Tanh)
+        q_scale = keep.tile([P, 1], F32, name="q_scale")
+        nc.vector.tensor_mul(out=q_scale[:], in0=b_tanh[:], in1=b_roots[:, 1:2])
+        q_scale_x2 = keep.tile([P, 1], F32, name="q_scale_x2")
+        nc.vector.tensor_scalar_mul(out=q_scale_x2[:], in0=q_scale[:], scalar1=2.0)
+        q_scale_neg = keep.tile([P, 1], F32, name="q_scale_neg")
+        nc.vector.tensor_scalar_mul(out=q_scale_neg[:], in0=q_scale[:], scalar1=-1.0)
+        qq = keep.tile([P, 1], F32, name="qq")
+        nc.vector.tensor_scalar(
+            out=qq[:], in0=b_sum[:], scalar1=q_scale[:, 0:1], scalar2=q_scale[:, 0:1],
+            op0=ALU.mult, op1=ALU.mult,
+        )
+        qq_plus_1 = keep.tile([P, 1], F32, name="qq_plus_1")
+        nc.vector.tensor_scalar_add(out=qq_plus_1[:], in0=qq[:], scalar1=1.0)
+
+        w_codes = keep.tile([P, PASSES, N], U32, align_bytes=64, name="w_codes")
+        w_scales = keep.tile([P, PASSES, N], U8, align_bytes=64, name="w_scales")
+        for wp in range(N // PAIR):
+            cols = slice(PAIR * wp, PAIR * (wp + 1))
+            for g in range(PASSES):
+                transpose_and_quantise(
+                    nc, psum, stage, "bank%d" % (4 + (PASSES * wp + g) % 4),
+                    w_pairs[wp][:].bitcast(F32), g, ident, w_codes[:, g, cols], w_scales[:, g, cols],
+                )
+
+        mx_sq_sum = keep.tile([P, ROW_TILES, HALVES], F32, name="mx_sq_sum")
+        mx_q_sum = keep.tile([P, ROW_TILES, HALVES], F32, name="mx_q_sum")
+        mx = {}
+        for h in range(HALVES):
+            n_cols = slice(BANK * h, BANK * (h + 1))
+            for t in range(ROW_TILES):
+                acc = psum.tile([P, BANK], F32, tag="bank%d" % (ROW_TILES * h + t), name="acc")
+                for g in range(PASSES):
+                    nc.tensor.matmul_mx(
+                        out=acc[:],
+                        lhsT=x_codes[:, g, P * t : P * (t + 1)].bitcast(FP8X4),
+                        lhsT_scale=x_scales[:, g, P * t : P * (t + 1)],
+                        rhs=w_codes[:, g, n_cols].bitcast(FP8X4),
+                        rhs_scale=w_scales[:, g, n_cols],
+                        start=(g == 0),
+                        stop=(g == PASSES - 1),
+                    )
+                mx[(t, h)] = acc
+                mx_sq = junk.tile([P, BANK], BF16, name="mx_sq")
+                nc.scalar.activation(
+                    out=mx_sq[:], in_=acc[:], func=ACT.Square, accum_out=mx_sq_sum[:, t, h : h + 1]
+                )
+                mx_q = junk.tile([P, BANK], F32, name="mx_q")
+                nc.vector.scalar_tensor_tensor(
+                    out=mx_q[:], in0=acc[:], scalar=q_scale_x2[:, 0:1], in1=b_all[:, n_cols],
+                    op0=ALU.mult, op1=ALU.mult, accum_out=mx_q_sum[:, t, h : h + 1],
+                )
+
+        for t in range(ROW_TILES):
+            s = small.tile([P, 1], F32, name="s")
+            nc.vector.tensor_scalar(
+                out=s[:], in0=mx_sq_sum[:, t, 0:1], scalar1=mx_sq_sum[:, t, 1:2], scalar2=EPS,
+                op0=ALU.add, op1=ALU.max,
+            )
+            roots = small.tile([P, 2], F32, name="roots")
+            nc.gpsimd.tensor_tensor(
+                out=roots[:], in0=s[:, 0:1].to_broadcast([P, 2]), in1=exp_pair[:], op=ALU.pow
+            )
+            th = small.tile([P, 1], F32, name="th")
+            nc.scalar.activation(
+                out=th[:], in_=roots[:, 0:1], func=ACT.Tanh, scale=gain[:, t : t + 1]
+            )
+            w = small.tile([P, 1], F32, name="w")
+            nc.vector.tensor_scalar(
+                out=w[:], in0=mx_q_sum[:, t, 0:1], scalar1=mx_q_sum[:, t, 1:2], scalar2=roots[:, 1:2],
+                op0=ALU.add, op1=ALU.mult,
+            )
+            a_ = small.tile([P, 1], F32, name="a_")
+            nc.vector.tensor_scalar(
+                out=a_[:], in0=th[:], scalar1=w[:, 0:1], scalar2=qq_plus_1[:, 0:1],
+                op0=ALU.mult, op1=ALU.add,
+            )
+            neg_b = small.tile([P, 1], F32, name="neg_b")
+            nc.vector.tensor_scalar(
+                out=neg_b[:], in0=th[:], scalar1=th[:, 0:1], scalar2=1.0,
+                op0=ALU.mult, op1=ALU.subtract,
+            )
+            den = small.tile([P, 1], F32, name="den")
+            nc.vector.tensor_scalar(
+                out=den[:], in0=neg_b[:], scalar1=qq[:, 0:1], scalar2=a_[:, 0:1],
+                op0=ALU.mult, op1=ALU.add,
+            )
+            nn = small.tile([P, 1], F32, name="nn")
+            nc.vector.tensor_scalar(
+                out=nn[:], in0=a_[:], scalar1=neg_b[:, 0:1], scalar2=1.0 / (MAXN * MAXN),
+                op0=ALU.add, op1=ALU.mult,
+            )
+            big = small.tile([P, 1], F32, name="big")
+            nc.vector.tensor_scalar(
+                out=big[:], in0=den[:], scalar1=EPS, scalar2=nn[:, 0:1], op0=ALU.max, op1=ALU.max
+            )
+            prod = small.tile([P, 1], F32, name="prod")
+            nc.vector.tensor_scalar(
+                out=prod[:], in0=den[:], scalar1=EPS, scalar2=big[:, 0:1], op0=ALU.max, op1=ALU.mult
+            )
+            f = small.tile([P, 1], F32, name="f")
+            nc.gpsimd.tensor_tensor(out=f[:], in0=prod[:], in1=exp_pair[:, 1:2], op=ALU.pow)
+            a_r = small.tile([P, 1], F32, name="a_r")
+            nc.vector.tensor_scalar(
+                out=a_r[:], in0=a_[:], scalar1=th[:, 0:1], scalar2=roots[:, 1:2],
+                op0=ALU.mult, op1=ALU.mult,
+            )
+            coef_mx = small.tile([P, 1], F32, name="coef_mx")
+            nc.vector.tensor_mul(out=coef_mx[:], in0=a_r[:], in1=f[:])
+            coef_b = small.tile([P, 1], F32, name="coef_b")
+            nc.vector.tensor_scalar(
+                out=coef_b[:], in0=neg_b[:], scalar1=f[:, 0:1], scalar2=q_scale_neg[:, 0:1],
+                op0=ALU.mult, op1=ALU.mult,
+            )
+
+            b_term = rows_out.tile([P, N], F32, name="b_term")
+            nc.scalar.activation(out=b_term[:], in_=b_all[:], func=ACT.Copy, scale=coef_b[:, 0:1])
+            result = rows_out.tile([P, N], F32, name="result")
+            for h in range(HALVES):
+                n_cols = slice(BANK * h, BANK * (h + 1))
+                nc.vector.scalar_tensor_tensor(
+                    out=result[:, n_cols], in0=mx[(t, h)][:], scalar=coef_mx[:, 0:1],
+                    in1=b_term[:, n_cols], op0=ALU.mult, op1=ALU.add,
+                )
+            xp, a = divmod(t, 2)
+            nc.sync.dma_start(
+                out=out[PAIR * xp : PAIR * (xp + 1), :].rearrange("(p a) n -> p a n", a=2)[:, a, :],
+                in_=result[:],
+            )

@@ -1,3 +1,5 @@
+import functools
+import math
 from contextlib import ExitStack
 
 import concourse.mybir as mybir
@@ -16,264 +18,476 @@ P = 128
 ROWS = 512
 K = 1024
 N = 1024
-K_PASS = 4 * P
-PASSES = K // K_PASS
-PAIR = 2 * P
-ROW_TILES = ROWS // P
+PASSES = K // (4 * P)
+X_BLOCKS = ROWS // P
+W_BLOCKS = N // P
 BANK = 512
 HALVES = N // BANK
-WORDS = K // 2
+BLOCKS_PER_HALF = W_BLOCKS // HALVES
 
 EPS = 1e-15
 MAXN = 1.0 - 1e-5
+EDGE = 1.5 - 0.5 / (MAXN * MAXN)
 FLOPS = 2 * ROWS * K * N
 
-
-def transpose_and_quantise(nc, psum, stage, bank_tag, pair_words, g, ident, codes, scales):
-    flipped = psum.tile([P, 2, PAIR], F32, tag=bank_tag, name="flipped")
-    for u in range(2):
-        for a in range(2):
-            first = WORDS * a + 2 * P * g + P * u
-            nc.tensor.transpose(
-                flipped[:, u, P * a : P * (a + 1)], pair_words[:, first : first + P], ident[:]
-            )
-    grouped = stage.tile([P, 4 * PAIR], BF16, align_bytes=64, name="grouped")
-    nc.scalar.copy(
-        out=grouped[:].bitcast(F32).rearrange("p (c u) -> p c u", u=2),
-        in_=flipped[:].rearrange("p u c -> p c u"),
-    )
-    nc.vector.quantize_mx(out=codes.bitcast(FP8X4), scales=scales, in_=grouped[:])
+SEED_MASK = 0x7FFFFFFF
+SEED = 2.0 / (math.sqrt(2.0) + 8.0 / (3.0 * math.sqrt(3.0))) * 2.0 ** -65
 
 
 def tile_directnodecomphyperbolicforecaster_pa_kernel(tc, v_init, W_vel, b_vel, out):
     nc = tc.nc
     with ExitStack() as ctx:
+        ctx.enter_context(tc.manual_schedule())
         keep = ctx.enter_context(tc.tile_pool(name="keep", bufs=1))
-        stage = ctx.enter_context(tc.tile_pool(name="stage", bufs=4))
-        junk = ctx.enter_context(tc.tile_pool(name="junk", bufs=2))
-        small = ctx.enter_context(tc.tile_pool(name="small", bufs=ROW_TILES))
-        rows_out = ctx.enter_context(tc.tile_pool(name="rows_out", bufs=ROW_TILES))
         psum = ctx.enter_context(tc.psum_pool(name="psum", bufs=1))
 
+        def wide(name, width):
+            return keep.tile([P, width], F32, name=name)
+
+        b_cols = keep.tile([P, N // P], BF16, name="b_cols")
+        nc.scalar.dma_start(out=b_cols[:], in_=b_vel.rearrange("(p j) -> p j", p=P))
+        blocks = []
+        for i in range(X_BLOCKS + W_BLOCKS):
+            rows = keep.tile([P, K], BF16, name="rows%d" % i)
+            if i < X_BLOCKS:
+                source = v_init[P * i : P * (i + 1), :]
+            else:
+                source = W_vel[P * (i - X_BLOCKS) : P * (i - X_BLOCKS + 1), :]
+            nc.sync.dma_start(out=rows[:], in_=source)
+            blocks.append(rows)
         b_row0 = keep.tile([P, N], BF16, name="b_row0")
+        first = wide("first", 1)
+        nc.vector.memset(first[:], 1.0)
         nc.vector.memset(b_row0[:].bitcast(I32), 0)
-        nc.sync.dma_start(out=b_row0[0:1, :], in_=b_vel.rearrange("(o n) -> o n", o=1))
+        nc.scalar.dma_start(out=b_row0[0:1, :], in_=b_vel.rearrange("(o n) -> o n", o=1))
 
-        x_pairs = []
-        for xp in range(ROWS // PAIR):
-            x_pair = keep.tile([P, 2 * K], BF16, name="x_pair%d" % xp)
-            nc.sync.dma_start(
-                out=x_pair[:].rearrange("p (a k) -> p a k", a=2),
-                in_=v_init[PAIR * xp : PAIR * (xp + 1), :].rearrange("(p a) k -> p a k", a=2),
-            )
-            x_pairs.append(x_pair)
-        w_pairs = []
-        for wp in range(N // PAIR):
-            w_pair = keep.tile([P, 2 * K], BF16, name="w_pair%d" % wp)
-            nc.sync.dma_start(
-                out=w_pair[:].rearrange("p (a k) -> p a k", a=2),
-                in_=W_vel[PAIR * wp : PAIR * (wp + 1), :].rearrange("(a p) k -> p a k", p=P),
-            )
-            w_pairs.append(w_pair)
-
-        ident = keep.tile([P, P], F32, name="ident")
+        log_table = wide("log_table", 1)
+        nc.scalar.activation(out=log_table[:], in_=first[:], func=ACT.Ln)
+        ident = wide("ident", P)
         make_identity(nc, ident[:])
+        half = wide("half", 2)
+        nc.gpsimd.memset(half[:], 0.5)
         ones = keep.tile([P, P], BF16, name="ones")
         nc.vector.memset(ones[:], 1.0)
-        exp_pair = keep.tile([P, 2], F32, name="exp_pair")
-        nc.vector.memset(exp_pair[:, 0:1], 0.5)
-        nc.vector.memset(exp_pair[:, 1:2], -0.5)
-        exp_half = keep.tile([P, ROW_TILES], F32, name="exp_half")
-        nc.vector.memset(exp_half[:], 0.5)
-        exp_neg_half = keep.tile([P, ROW_TILES], F32, name="exp_neg_half")
-        nc.vector.memset(exp_neg_half[:], -0.5)
+        ones_f = wide("ones_f", P)
+        nc.vector.memset(ones_f[:], 1.0)
 
-        b_psum = psum.tile([P, N], BF16, tag="bank7", name="b_psum")
-        for h in range(HALVES):
-            cols = slice(BANK * h, BANK * (h + 1))
-            nc.tensor.matmul(b_psum[:, cols], lhsT=ones[:], rhs=b_row0[:, cols], start=True, stop=True)
-        b_sq = junk.tile([P, N], BF16, name="b_sq")
-        b_sum = keep.tile([P, 1], F32, name="b_sum")
-        nc.scalar.activation(out=b_sq[:], in_=b_psum[:], func=ACT.Square, accum_out=b_sum[:])
-        b_all = keep.tile([P, N], BF16, name="b_all")
-        nc.scalar.copy(out=b_all[:], in_=b_psum[:])
-
-        x_codes = keep.tile([P, PASSES, ROWS], U32, align_bytes=64, name="x_codes")
-        x_scales = keep.tile([P, PASSES, ROWS], U8, align_bytes=64, name="x_scales")
-        x_sum = keep.tile([P, ROW_TILES], F32, name="x_sum")
-        for xp in range(ROWS // PAIR):
-            cols = slice(PAIR * xp, PAIR * (xp + 1))
-            for g in range(PASSES):
-                transpose_and_quantise(
-                    nc, psum, stage, "bank%d" % (PASSES * xp + g), x_pairs[xp][:].bitcast(F32), g,
-                    ident, x_codes[:, g, cols], x_scales[:, g, cols],
-                )
-            for a in range(2):
-                x_sq = junk.tile([P, K], F32, name="x_sq")
-                x_rows = x_pairs[xp][:, K * a : K * (a + 1)]
-                nc.vector.scalar_tensor_tensor(
-                    out=x_sq[:], in0=x_rows, scalar=1.0, in1=x_rows, op0=ALU.mult, op1=ALU.mult,
-                    accum_out=x_sum[:, 2 * xp + a : 2 * xp + a + 1],
-                )
-
-        x_sum_c = keep.tile([P, ROW_TILES], F32, name="x_sum_c")
-        nc.vector.tensor_scalar_max(out=x_sum_c[:], in0=x_sum[:], scalar1=EPS)
-        xn = keep.tile([P, ROW_TILES], F32, name="xn")
-        nc.gpsimd.tensor_tensor(out=xn[:], in0=x_sum_c[:], in1=exp_half[:], op=ALU.pow)
-        xn_inv = keep.tile([P, ROW_TILES], F32, name="xn_inv")
-        nc.gpsimd.tensor_tensor(out=xn_inv[:], in0=x_sum_c[:], in1=exp_neg_half[:], op=ALU.pow)
-        clipped = keep.tile([P, ROW_TILES], F32, name="clipped")
-        nc.vector.tensor_scalar_min(out=clipped[:], in0=xn[:], scalar1=1.0 - 1e-7)
-        one_minus = keep.tile([P, ROW_TILES], F32, name="one_minus")
-        nc.vector.tensor_scalar(
-            out=one_minus[:], in0=clipped[:], scalar1=-1.0, scalar2=1.0, op0=ALU.mult, op1=ALU.add
-        )
-        one_minus_inv = keep.tile([P, ROW_TILES], F32, name="one_minus_inv")
-        nc.vector.reciprocal(out=one_minus_inv[:], in_=one_minus[:])
-        ratio = keep.tile([P, ROW_TILES], F32, name="ratio")
-        nc.vector.scalar_tensor_tensor(
-            out=ratio[:], in0=clipped[:], scalar=1.0, in1=one_minus_inv[:], op0=ALU.add, op1=ALU.mult
-        )
-        log_ratio = keep.tile([P, ROW_TILES], F32, name="log_ratio")
-        nc.scalar.activation(out=log_ratio[:], in_=ratio[:], func=ACT.Ln)
-        gain = keep.tile([P, ROW_TILES], F32, name="gain")
-        nc.vector.scalar_tensor_tensor(
-            out=gain[:], in0=log_ratio[:], scalar=0.5, in1=xn_inv[:], op0=ALU.mult, op1=ALU.mult
-        )
-
-        b_sum_c = keep.tile([P, 1], F32, name="b_sum_c")
-        nc.vector.tensor_scalar_max(out=b_sum_c[:], in0=b_sum[:], scalar1=EPS)
-        b_roots = keep.tile([P, 2], F32, name="b_roots")
-        nc.gpsimd.tensor_tensor(
-            out=b_roots[:], in0=b_sum_c[:, 0:1].to_broadcast([P, 2]), in1=exp_pair[:], op=ALU.pow
-        )
-        b_tanh = keep.tile([P, 1], F32, name="b_tanh")
-        nc.scalar.activation(out=b_tanh[:], in_=b_roots[:, 0:1], func=ACT.Tanh)
-        q_scale = keep.tile([P, 1], F32, name="q_scale")
-        nc.vector.tensor_mul(out=q_scale[:], in0=b_tanh[:], in1=b_roots[:, 1:2])
-        q_scale_x2 = keep.tile([P, 1], F32, name="q_scale_x2")
-        nc.vector.tensor_scalar_mul(out=q_scale_x2[:], in0=q_scale[:], scalar1=2.0)
-        q_scale_neg = keep.tile([P, 1], F32, name="q_scale_neg")
-        nc.vector.tensor_scalar_mul(out=q_scale_neg[:], in0=q_scale[:], scalar1=-1.0)
-        qq = keep.tile([P, 1], F32, name="qq")
-        nc.vector.tensor_scalar(
-            out=qq[:], in0=b_sum[:], scalar1=q_scale[:, 0:1], scalar2=q_scale[:, 0:1],
-            op0=ALU.mult, op1=ALU.mult,
-        )
-        qq_plus_1 = keep.tile([P, 1], F32, name="qq_plus_1")
-        nc.vector.tensor_scalar_add(out=qq_plus_1[:], in0=qq[:], scalar1=1.0)
-
+        x_codes = keep.tile([P, X_BLOCKS * PASSES * P], U32, align_bytes=64, name="x_codes")
+        x_scales = keep.tile([P, X_BLOCKS * PASSES * P], U8, align_bytes=64, name="x_scales")
         w_codes = keep.tile([P, PASSES, N], U32, align_bytes=64, name="w_codes")
         w_scales = keep.tile([P, PASSES, N], U8, align_bytes=64, name="w_scales")
-        for wp in range(N // PAIR):
-            cols = slice(PAIR * wp, PAIR * (wp + 1))
+        sums = wide("sums", X_BLOCKS + 1)
+        flipped = {}
+        grouped = {}
+
+        def turn(i):
+            words = blocks[i][:].bitcast(F32)
+            bank = i if i < 8 else i - 4
+            f = psum.tile([P, PASSES, 2, P], F32, tag="bank%d" % bank, name="flipped")
             for g in range(PASSES):
-                transpose_and_quantise(
-                    nc, psum, stage, "bank%d" % (4 + (PASSES * wp + g) % 4),
-                    w_pairs[wp][:].bitcast(F32), g, ident, w_codes[:, g, cols], w_scales[:, g, cols],
-                )
+                for u in range(2):
+                    start = P * (2 * g + u)
+                    nc.tensor.transpose(f[:, g, u, :], words[:, start : start + P], ident[:])
+            flipped[i] = f
 
-        mx_sq_sum = keep.tile([P, ROW_TILES, HALVES], F32, name="mx_sq_sum")
-        mx_q_sum = keep.tile([P, ROW_TILES, HALVES], F32, name="mx_q_sum")
-        mx = {}
-        for h in range(HALVES):
-            n_cols = slice(BANK * h, BANK * (h + 1))
-            for t in range(ROW_TILES):
-                acc = psum.tile([P, BANK], F32, tag="bank%d" % (ROW_TILES * h + t), name="acc")
+        def evacuate(i):
+            t = keep.tile([P, PASSES * 4 * P], BF16, align_bytes=64, name="grouped%d" % i)
+            nc.scalar.copy(
+                out=t[:].bitcast(F32).rearrange("p (g c u) -> p g c u", g=PASSES, u=2),
+                in_=flipped[i][:].rearrange("p g u c -> p g c u"),
+            )
+            grouped[i] = t
+
+        def quantise(i):
+            if i < X_BLOCKS:
+                cols = slice(PASSES * P * i, PASSES * P * (i + 1))
+                nc.vector.quantize_mx(
+                    out=x_codes[:, cols].bitcast(FP8X4), scales=x_scales[:, cols], in_=grouped[i][:]
+                )
+            else:
+                cols = slice(P * (i - X_BLOCKS), P * (i - X_BLOCKS + 1))
                 for g in range(PASSES):
-                    nc.tensor.matmul_mx(
-                        out=acc[:],
-                        lhsT=x_codes[:, g, P * t : P * (t + 1)].bitcast(FP8X4),
-                        lhsT_scale=x_scales[:, g, P * t : P * (t + 1)],
-                        rhs=w_codes[:, g, n_cols].bitcast(FP8X4),
-                        rhs_scale=w_scales[:, g, n_cols],
-                        start=(g == 0),
-                        stop=(g == PASSES - 1),
+                    nc.vector.quantize_mx(
+                        out=w_codes[:, g, cols].bitcast(FP8X4), scales=w_scales[:, g, cols],
+                        in_=grouped[i][:, 4 * P * g : 4 * P * (g + 1)],
                     )
-                mx[(t, h)] = acc
-                mx_sq = junk.tile([P, BANK], BF16, name="mx_sq")
-                nc.scalar.activation(
-                    out=mx_sq[:], in_=acc[:], func=ACT.Square, accum_out=mx_sq_sum[:, t, h : h + 1]
-                )
-                mx_q = junk.tile([P, BANK], F32, name="mx_q")
-                nc.vector.scalar_tensor_tensor(
-                    out=mx_q[:], in0=acc[:], scalar=q_scale_x2[:, 0:1], in1=b_all[:, n_cols],
-                    op0=ALU.mult, op1=ALU.mult, accum_out=mx_q_sum[:, t, h : h + 1],
-                )
 
-        for t in range(ROW_TILES):
-            s = small.tile([P, 1], F32, name="s")
-            nc.vector.tensor_scalar(
-                out=s[:], in0=mx_sq_sum[:, t, 0:1], scalar1=mx_sq_sum[:, t, 1:2], scalar2=EPS,
-                op0=ALU.add, op1=ALU.max,
-            )
-            roots = small.tile([P, 2], F32, name="roots")
-            nc.gpsimd.tensor_tensor(
-                out=roots[:], in0=s[:, 0:1].to_broadcast([P, 2]), in1=exp_pair[:], op=ALU.pow
-            )
-            th = small.tile([P, 1], F32, name="th")
-            nc.scalar.activation(
-                out=th[:], in_=roots[:, 0:1], func=ACT.Tanh, scale=gain[:, t : t + 1]
-            )
-            w = small.tile([P, 1], F32, name="w")
-            nc.vector.tensor_scalar(
-                out=w[:], in0=mx_q_sum[:, t, 0:1], scalar1=mx_q_sum[:, t, 1:2], scalar2=roots[:, 1:2],
-                op0=ALU.add, op1=ALU.mult,
-            )
-            a_ = small.tile([P, 1], F32, name="a_")
-            nc.vector.tensor_scalar(
-                out=a_[:], in0=th[:], scalar1=w[:, 0:1], scalar2=qq_plus_1[:, 0:1],
-                op0=ALU.mult, op1=ALU.add,
-            )
-            neg_b = small.tile([P, 1], F32, name="neg_b")
-            nc.vector.tensor_scalar(
-                out=neg_b[:], in0=th[:], scalar1=th[:, 0:1], scalar2=1.0,
-                op0=ALU.mult, op1=ALU.subtract,
-            )
-            den = small.tile([P, 1], F32, name="den")
-            nc.vector.tensor_scalar(
-                out=den[:], in0=neg_b[:], scalar1=qq[:, 0:1], scalar2=a_[:, 0:1],
-                op0=ALU.mult, op1=ALU.add,
-            )
-            nn = small.tile([P, 1], F32, name="nn")
-            nc.vector.tensor_scalar(
-                out=nn[:], in0=a_[:], scalar1=neg_b[:, 0:1], scalar2=1.0 / (MAXN * MAXN),
-                op0=ALU.add, op1=ALU.mult,
-            )
-            big = small.tile([P, 1], F32, name="big")
-            nc.vector.tensor_scalar(
-                out=big[:], in0=den[:], scalar1=EPS, scalar2=nn[:, 0:1], op0=ALU.max, op1=ALU.max
-            )
-            prod = small.tile([P, 1], F32, name="prod")
-            nc.vector.tensor_scalar(
-                out=prod[:], in0=den[:], scalar1=EPS, scalar2=big[:, 0:1], op0=ALU.max, op1=ALU.mult
-            )
-            f = small.tile([P, 1], F32, name="f")
-            nc.gpsimd.tensor_tensor(out=f[:], in0=prod[:], in1=exp_pair[:, 1:2], op=ALU.pow)
-            a_r = small.tile([P, 1], F32, name="a_r")
-            nc.vector.tensor_scalar(
-                out=a_r[:], in0=a_[:], scalar1=th[:, 0:1], scalar2=roots[:, 1:2],
-                op0=ALU.mult, op1=ALU.mult,
-            )
-            coef_mx = small.tile([P, 1], F32, name="coef_mx")
-            nc.vector.tensor_mul(out=coef_mx[:], in0=a_r[:], in1=f[:])
-            coef_b = small.tile([P, 1], F32, name="coef_b")
-            nc.vector.tensor_scalar(
-                out=coef_b[:], in0=neg_b[:], scalar1=f[:, 0:1], scalar2=q_scale_neg[:, 0:1],
-                op0=ALU.mult, op1=ALU.mult,
+        def square_rows(i):
+            sq = keep.tile([P, K], BF16, name="x_sq%d" % i)
+            nc.vector.scalar_tensor_tensor(
+                out=sq[:], in0=blocks[i][:], scalar=1.0, in1=blocks[i][:], op0=ALU.mult,
+                op1=ALU.mult, accum_out=sums[:, i : i + 1],
             )
 
-            b_term = rows_out.tile([P, N], F32, name="b_term")
-            nc.scalar.activation(out=b_term[:], in_=b_all[:], func=ACT.Copy, scale=coef_b[:, 0:1])
-            result = rows_out.tile([P, N], F32, name="result")
-            for h in range(HALVES):
+        mx = {}
+        mx_sq = keep.tile([P, HALVES, X_BLOCKS], F32, name="mx_sq")
+        mx_b = keep.tile([P, HALVES, X_BLOCKS], F32, name="mx_b")
+
+        def multiply(h, t):
+            acc = psum.tile([P, BANK], F32, tag="bank%d" % (X_BLOCKS * h + t), name="acc")
+            for g in range(PASSES):
+                x_cols = slice(P * (PASSES * t + g), P * (PASSES * t + g + 1))
                 n_cols = slice(BANK * h, BANK * (h + 1))
-                nc.vector.scalar_tensor_tensor(
-                    out=result[:, n_cols], in0=mx[(t, h)][:], scalar=coef_mx[:, 0:1],
-                    in1=b_term[:, n_cols], op0=ALU.mult, op1=ALU.add,
+                nc.tensor.matmul_mx(
+                    out=acc[:],
+                    lhsT=x_codes[:, x_cols].bitcast(FP8X4), lhsT_scale=x_scales[:, x_cols],
+                    rhs=w_codes[:, g, n_cols].bitcast(FP8X4), rhs_scale=w_scales[:, g, n_cols],
+                    start=(g == 0), stop=(g == PASSES - 1),
                 )
-            xp, a = divmod(t, 2)
-            nc.sync.dma_start(
-                out=out[PAIR * xp : PAIR * (xp + 1), :].rearrange("(p a) n -> p a n", a=2)[:, a, :],
-                in_=result[:],
+            mx[(h, t)] = acc
+
+        def square_mx(h, t):
+            junk = keep.tile([P, BANK], BF16, name="junk_s%d%d" % (h, t))
+            nc.scalar.activation(
+                out=junk[:], in_=mx[(h, t)][:], func=ACT.Square, accum_out=mx_sq[:, h, t : t + 1]
             )
+
+        b_all = keep.tile([P, N], BF16, name="b_all")
+
+        def dot_mx(h, t):
+            junk = keep.tile([P, BANK], BF16, name="junk_d%d%d" % (h, t))
+            nc.vector.scalar_tensor_tensor(
+                out=junk[:], in0=mx[(h, t)][:], scalar=1.0, in1=b_all[:, BANK * h : BANK * (h + 1)],
+                op0=ALU.mult, op1=ALU.mult, accum_out=mx_b[:, h, t : t + 1],
+            )
+
+        width = X_BLOCKS + 1
+        sums_c = wide("sums_c", width)
+        guess = keep.tile([P, width], I32, name="guess")
+        g = [wide("g%d" % j, width)[:] for j in range(4)]
+        y = [guess[:].bitcast(F32)] + [wide("y%d" % j, width)[:] for j in range(1, 4)]
+        r = [wide("r%d" % j, width)[:] for j in range(3)]
+        clipped = wide("clipped", X_BLOCKS)
+        one_minus = wide("one_minus", X_BLOCKS)
+        one_minus_inv = wide("one_minus_inv", X_BLOCKS)
+        ratio = wide("ratio", X_BLOCKS)
+        stt = nc.vector.scalar_tensor_tensor
+        steps = [
+            functools.partial(nc.vector.tensor_scalar_max, out=sums_c[:], in0=sums[:], scalar1=EPS),
+            functools.partial(
+                nc.vector.tensor_scalar, out=guess[:], in0=sums_c[:].bitcast(I32), scalar1=1,
+                scalar2=SEED_MASK, op0=ALU.logical_shift_right, op1=ALU.bitwise_xor,
+            ),
+            functools.partial(
+                stt, out=g[0], in0=y[0], scalar=SEED, in1=sums_c[:], op0=ALU.mult, op1=ALU.mult
+            ),
+        ]
+        for j in range(3):
+            steps += [
+                functools.partial(
+                    stt, out=r[j], in0=g[j], scalar=-0.5 * SEED, in1=y[j], op0=ALU.mult, op1=ALU.mult
+                ),
+                functools.partial(
+                    stt, out=g[j + 1], in0=r[j], scalar=1.5, in1=g[j], op0=ALU.add, op1=ALU.mult
+                ),
+                functools.partial(
+                    stt, out=y[j + 1], in0=r[j], scalar=1.5, in1=y[j], op0=ALU.add, op1=ALU.mult
+                ),
+            ]
+        steps += [
+            functools.partial(
+                nc.vector.tensor_scalar_min, out=clipped[:], in0=g[3][:, 0:X_BLOCKS], scalar1=1.0 - 1e-7
+            ),
+            functools.partial(
+                nc.vector.tensor_scalar, out=one_minus[:], in0=clipped[:], scalar1=-1.0, scalar2=1.0,
+                op0=ALU.mult, op1=ALU.add,
+            ),
+            functools.partial(nc.vector.reciprocal, out=one_minus_inv[:], in_=one_minus[:]),
+            functools.partial(
+                stt, out=ratio[:], in0=clipped[:], scalar=1.0, in1=one_minus_inv[:], op0=ALU.add,
+                op1=ALU.mult,
+            ),
+        ]
+
+        def advance(count):
+            for step in steps[:count]:
+                step()
+            for step in steps[:count]:
+                steps.remove(step)
+
+        turn(0)
+        evacuate(0)
+        square_rows(0)
+        turn(1)
+        evacuate(1)
+        quantise(0)
+        b_sq = wide("b_sq", N // P)
+        b_part = wide("b_part", 1)
+        stt(
+            out=b_sq[:], in0=b_cols[:], scalar=1.0, in1=b_cols[:], op0=ALU.mult, op1=ALU.mult,
+            accum_out=b_part[:],
+        )
+        turn(2)
+        evacuate(2)
+        square_rows(1)
+        quantise(1)
+        turn(3)
+        evacuate(3)
+        quantise(2)
+        b_tot = psum.tile([P, 1], F32, tag="bank0", name="b_tot")
+        nc.tensor.matmul(b_tot[:], lhsT=ones_f[:], rhs=b_part[:], start=True, stop=True)
+        turn(4)
+        evacuate(4)
+        nc.vector.tensor_copy(out=sums[:, X_BLOCKS : X_BLOCKS + 1], in_=b_tot[:])
+        square_rows(2)
+        quantise(3)
+        turn(5)
+        evacuate(5)
+        quantise(4)
+        b_psum = psum.tile([P, N], BF16, tag="bank1", name="b_psum")
+
+        def spread_bias(h):
+            cols = slice(BANK * h, BANK * (h + 1))
+            nc.tensor.matmul(b_psum[:, cols], lhsT=ones[:], rhs=b_row0[:, cols], start=True, stop=True)
+
+        spread_bias(0)
+        square_rows(3)
+        turn(6)
+        evacuate(6)
+        advance(1)
+        quantise(5)
+        turn(7)
+        evacuate(7)
+        spread_bias(1)
+        advance(1)
+        quantise(6)
+        advance(2)
+        turn(8)
+        evacuate(8)
+        quantise(7)
+        advance(3)
+        nc.scalar.copy(out=b_all[:], in_=b_psum[:])
+        turn(9)
+        evacuate(9)
+        quantise(8)
+        advance(3)
+        turn(10)
+        evacuate(10)
+        quantise(9)
+        advance(3)
+        turn(11)
+        evacuate(11)
+        for t in range(X_BLOCKS):
+            multiply(0, t)
+        quantise(10)
+        advance(2)
+        square_mx(0, 0)
+        quantise(11)
+        advance(1)
+        for t in range(X_BLOCKS):
+            multiply(1, t)
+        dot_mx(0, 1)
+        dot_mx(0, 0)
+        log_ratio = wide("log_ratio", X_BLOCKS)
+        nc.scalar.activation(out=log_ratio[:], in_=ratio[:], func=ACT.Ln)
+        b_tanh = wide("b_tanh", 1)
+        nc.scalar.activation(out=b_tanh[:], in_=g[3][:, X_BLOCKS : X_BLOCKS + 1], func=ACT.Tanh)
+        square_mx(0, 1)
+        dot_mx(1, 0)
+        square_mx(1, 0)
+        dot_mx(1, 1)
+        gain = wide("gain", X_BLOCKS)
+        stt(
+            out=gain[:], in0=log_ratio[:], scalar=0.5 * SEED, in1=y[3][:, 0:X_BLOCKS],
+            op0=ALU.mult, op1=ALU.mult,
+        )
+        square_mx(1, 1)
+        q_scale = wide("q_scale", 1)
+        nc.vector.tensor_scalar(
+            out=q_scale[:], in0=b_tanh[:], scalar1=y[3][:, X_BLOCKS : X_BLOCKS + 1], scalar2=SEED,
+            op0=ALU.mult, op1=ALU.mult,
+        )
+        q_twice = wide("q_twice", 1)
+        nc.vector.tensor_scalar_mul(out=q_twice[:], in0=q_scale[:], scalar1=2.0)
+        q_neg = wide("q_neg", 1)
+        nc.vector.tensor_scalar_mul(out=q_neg[:], in0=q_scale[:], scalar1=-1.0)
+        qq = wide("qq", 1)
+        nc.vector.tensor_scalar(
+            out=qq[:], in0=sums[:, X_BLOCKS : X_BLOCKS + 1], scalar1=q_scale[:, 0:1],
+            scalar2=q_scale[:, 0:1], op0=ALU.mult, op1=ALU.mult,
+        )
+        qq_plus_1 = wide("qq_plus_1", 1)
+        nc.vector.tensor_scalar_add(out=qq_plus_1[:], in0=qq[:], scalar1=1.0)
+        edge_scale = wide("edge_scale", 1)
+        nc.vector.tensor_scalar(
+            out=edge_scale[:], in0=qq[:], scalar1=0.5 / (MAXN * MAXN), scalar2=-0.5 / (MAXN * MAXN),
+            op0=ALU.mult, op1=ALU.add,
+        )
+
+        s = wide("s", X_BLOCKS)
+        mxn = wide("mxn", X_BLOCKS)
+        inv_mxn = wide("inv_mxn", X_BLOCKS)
+        th = wide("th", X_BLOCKS)
+        d = wide("d", X_BLOCKS)
+        w = wide("w", X_BLOCKS)
+        v = wide("v", X_BLOCKS)
+        t1 = wide("t1", X_BLOCKS)
+        p2 = wide("p2", X_BLOCKS)
+        den_1 = wide("den_1", X_BLOCKS)
+        thi = wide("thi", X_BLOCKS)
+        cbq = wide("cbq", X_BLOCKS)
+        den = wide("den", X_BLOCKS)
+        edge = wide("edge", X_BLOCKS)
+        ar = wide("ar", X_BLOCKS)
+        inv = wide("inv", X_BLOCKS)
+        shrink_den = wide("shrink_den", X_BLOCKS)
+        shrink = wide("shrink", X_BLOCKS)
+        ari = wide("ari", X_BLOCKS)
+        cbi = wide("cbi", X_BLOCKS)
+        coef_b = wide("coef_b", X_BLOCKS)
+        coef_mx = wide("coef_mx", X_BLOCKS)
+
+        def sum_squares(c):
+            for t in range(c.start, c.stop):
+                nc.vector.tensor_scalar(
+                    out=s[:, t : t + 1], in0=mx_sq[:, 0, t : t + 1], scalar1=mx_sq[:, 1, t : t + 1],
+                    scalar2=EPS, op0=ALU.add, op1=ALU.max,
+                )
+            nc.gpsimd.tensor_tensor(out=mxn[:, c], in0=s[:, c], in1=half[:], op=ALU.pow)
+
+        def tanhs(c):
+            for t in range(c.start, c.stop):
+                nc.scalar.activation(
+                    out=th[:, t : t + 1], in_=mxn[:, t : t + 1], func=ACT.Tanh, scale=gain[:, t : t + 1]
+                )
+
+        def dots(c):
+            nc.vector.tensor_add(out=d[:, c], in0=mx_b[:, 0, c], in1=mx_b[:, 1, c])
+
+        def inverse_norms(c):
+            nc.vector.reciprocal(out=inv_mxn[:, c], in_=mxn[:, c])
+
+        def weights(c):
+            stt(
+                out=w[:, c], in0=d[:, c], scalar=q_twice[:, 0:1], in1=inv_mxn[:, c], op0=ALU.mult,
+                op1=ALU.mult,
+            )
+
+        def coef_1(c):
+            stt(out=v[:, c], in0=th[:, c], scalar=qq[:, 0:1], in1=w[:, c], op0=ALU.mult, op1=ALU.add)
+            nc.vector.tensor_mul(out=t1[:, c], in0=th[:, c], in1=w[:, c])
+            nc.vector.tensor_mul(out=p2[:, c], in0=th[:, c], in1=th[:, c])
+
+        def coef_2(c):
+            nc.vector.tensor_mul(out=den_1[:, c], in0=v[:, c], in1=th[:, c])
+            nc.vector.tensor_mul(out=thi[:, c], in0=th[:, c], in1=inv_mxn[:, c])
+            nc.vector.tensor_scalar(
+                out=cbq[:, c], in0=p2[:, c], scalar1=1.0, scalar2=q_neg[:, 0:1], op0=ALU.subtract,
+                op1=ALU.mult,
+            )
+
+        def coef_3(c):
+            nc.vector.tensor_scalar(
+                out=den[:, c], in0=den_1[:, c], scalar1=1.0, scalar2=EPS, op0=ALU.add, op1=ALU.max
+            )
+            nc.vector.tensor_scalar(
+                out=edge[:, c], in0=p2[:, c], scalar1=1.0, scalar2=edge_scale[:, 0:1],
+                op0=ALU.subtract, op1=ALU.mult,
+            )
+            stt(
+                out=ar[:, c], in0=t1[:, c], scalar=qq_plus_1[:, 0:1], in1=thi[:, c], op0=ALU.add,
+                op1=ALU.mult,
+            )
+
+        def coef_4(c):
+            nc.vector.reciprocal(out=inv[:, c], in_=den[:, c])
+            stt(
+                out=shrink_den[:, c], in0=den[:, c], scalar=EDGE, in1=edge[:, c], op0=ALU.mult,
+                op1=ALU.add,
+            )
+
+        def coef_5(c):
+            nc.vector.tensor_mul(out=shrink[:, c], in0=shrink_den[:, c], in1=inv[:, c])
+            nc.vector.tensor_mul(out=cbi[:, c], in0=cbq[:, c], in1=inv[:, c])
+            nc.vector.tensor_mul(out=ari[:, c], in0=ar[:, c], in1=inv[:, c])
+
+        def coef_6(c):
+            for out_c, in_c in ((coef_b, cbi), (coef_mx, ari)):
+                stt(
+                    out=out_c[:, c], in0=shrink[:, c], scalar=1.0, in1=in_c[:, c], op0=ALU.min,
+                    op1=ALU.mult,
+                )
+
+        b_term = [wide("b_term%d" % t, N) for t in range(X_BLOCKS)]
+        result = [wide("result%d" % t, N) for t in range(X_BLOCKS)]
+
+        def bias(t, h):
+            cols = slice(BANK * h, BANK * (h + 1))
+            nc.scalar.activation(
+                out=b_term[t][:, cols], in_=b_all[:, cols], func=ACT.Copy, scale=coef_b[:, t : t + 1]
+            )
+
+        def bias_vector(t, h):
+            cols = slice(BANK * h, BANK * (h + 1))
+            nc.vector.tensor_scalar_mul(
+                out=b_term[t][:, cols], in0=b_all[:, cols], scalar1=coef_b[:, t : t + 1]
+            )
+
+        def bias_gpsimd(t, h):
+            cols = slice(BANK * h, BANK * (h + 1))
+            nc.gpsimd.tensor_scalar(
+                out=b_term[t][:, cols], in0=b_all[:, cols], scalar1=coef_b[:, t : t + 1], scalar2=0.0,
+                op0=ALU.mult, op1=ALU.add,
+            )
+
+        def finish(t, h):
+            cols = slice(BANK * h, BANK * (h + 1))
+            stt(
+                out=result[t][:, cols], in0=mx[(h, t)][:], scalar=coef_mx[:, t : t + 1],
+                in1=b_term[t][:, cols], op0=ALU.mult, op1=ALU.add,
+            )
+
+        def store(t):
+            nc.sync.dma_start(out=out[P * t : P * (t + 1), :], in_=result[t][:])
+
+        first_pair, second_pair = slice(0, 2), slice(2, 4)
+        dot_mx(0, 3)
+        dots(first_pair)
+        square_mx(0, 2)
+        sum_squares(first_pair)
+        dot_mx(0, 2)
+        square_mx(0, 3)
+        inverse_norms(first_pair)
+        weights(first_pair)
+        tanhs(first_pair)
+        dot_mx(1, 3)
+        square_mx(1, 2)
+        coef_1(first_pair)
+        coef_2(first_pair)
+        coef_3(first_pair)
+        square_mx(1, 3)
+        coef_4(first_pair)
+        coef_5(first_pair)
+        coef_6(first_pair)
+        bias(0, 0)
+        bias(0, 1)
+        dot_mx(1, 2)
+        dots(second_pair)
+        sum_squares(second_pair)
+        bias_gpsimd(1, 0)
+        finish(0, 0)
+        tanhs(second_pair)
+        bias(1, 1)
+        inverse_norms(second_pair)
+        finish(0, 1)
+        store(0)
+        weights(second_pair)
+        finish(1, 0)
+        coef_1(second_pair)
+        coef_2(second_pair)
+        coef_3(second_pair)
+        finish(1, 1)
+        store(1)
+        coef_4(second_pair)
+        coef_5(second_pair)
+        coef_6(second_pair)
+        bias_vector(2, 0)
+        bias(2, 1)
+        bias(3, 0)
+        bias_gpsimd(3, 1)
+        finish(2, 0)
+        finish(2, 1)
+        store(2)
+        finish(3, 0)
+        finish(3, 1)
+        store(3)

@@ -1,5 +1,3 @@
-import functools
-import math
 from contextlib import ExitStack
 
 import concourse.mybir as mybir
@@ -29,9 +27,6 @@ EPS = 1e-15
 MAXN = 1.0 - 1e-5
 EDGE = 1.5 - 0.5 / (MAXN * MAXN)
 FLOPS = 2 * ROWS * K * N
-
-SEED_MASK = 0x7FFFFFFF
-SEED = 2.0 / (math.sqrt(2.0) + 8.0 / (3.0 * math.sqrt(3.0))) * 2.0 ** -65
 
 
 def tile_directnodecomphyperbolicforecaster_pa_kernel(tc, v_init, W_vel, b_vel, out):
@@ -65,8 +60,10 @@ def tile_directnodecomphyperbolicforecaster_pa_kernel(tc, v_init, W_vel, b_vel, 
         nc.scalar.activation(out=log_table[:], in_=first[:], func=ACT.Ln)
         ident = wide("ident", P)
         make_identity(nc, ident[:])
-        half = wide("half", 2)
+        half = wide("half", X_BLOCKS + 1)
         nc.gpsimd.memset(half[:], 0.5)
+        neg_half = wide("neg_half", X_BLOCKS + 1)
+        nc.gpsimd.memset(neg_half[:], -0.5)
         ones = keep.tile([P, P], BF16, name="ones")
         nc.vector.memset(ones[:], 1.0)
         ones_f = wide("ones_f", P)
@@ -151,176 +148,15 @@ def tile_directnodecomphyperbolicforecaster_pa_kernel(tc, v_init, W_vel, b_vel, 
                 op0=ALU.mult, op1=ALU.mult, accum_out=mx_b[:, h, t : t + 1],
             )
 
-        width = X_BLOCKS + 1
-        sums_c = wide("sums_c", width)
-        guess = keep.tile([P, width], I32, name="guess")
-        g = [wide("g%d" % j, width)[:] for j in range(4)]
-        y = [guess[:].bitcast(F32)] + [wide("y%d" % j, width)[:] for j in range(1, 4)]
-        r = [wide("r%d" % j, width)[:] for j in range(3)]
-        clipped = wide("clipped", X_BLOCKS)
-        one_minus = wide("one_minus", X_BLOCKS)
-        one_minus_inv = wide("one_minus_inv", X_BLOCKS)
-        ratio = wide("ratio", X_BLOCKS)
         stt = nc.vector.scalar_tensor_tensor
-        steps = [
-            functools.partial(nc.vector.tensor_scalar_max, out=sums_c[:], in0=sums[:], scalar1=EPS),
-            functools.partial(
-                nc.vector.tensor_scalar, out=guess[:], in0=sums_c[:].bitcast(I32), scalar1=1,
-                scalar2=SEED_MASK, op0=ALU.logical_shift_right, op1=ALU.bitwise_xor,
-            ),
-            functools.partial(
-                stt, out=g[0], in0=y[0], scalar=SEED, in1=sums_c[:], op0=ALU.mult, op1=ALU.mult
-            ),
-        ]
-        for j in range(3):
-            steps += [
-                functools.partial(
-                    stt, out=r[j], in0=g[j], scalar=-0.5 * SEED, in1=y[j], op0=ALU.mult, op1=ALU.mult
-                ),
-                functools.partial(
-                    stt, out=g[j + 1], in0=r[j], scalar=1.5, in1=g[j], op0=ALU.add, op1=ALU.mult
-                ),
-                functools.partial(
-                    stt, out=y[j + 1], in0=r[j], scalar=1.5, in1=y[j], op0=ALU.add, op1=ALU.mult
-                ),
-            ]
-        steps += [
-            functools.partial(
-                nc.vector.tensor_scalar_min, out=clipped[:], in0=g[3][:, 0:X_BLOCKS], scalar1=1.0 - 1e-7
-            ),
-            functools.partial(
-                nc.vector.tensor_scalar, out=one_minus[:], in0=clipped[:], scalar1=-1.0, scalar2=1.0,
-                op0=ALU.mult, op1=ALU.add,
-            ),
-            functools.partial(nc.vector.reciprocal, out=one_minus_inv[:], in_=one_minus[:]),
-            functools.partial(
-                stt, out=ratio[:], in0=clipped[:], scalar=1.0, in1=one_minus_inv[:], op0=ALU.add,
-                op1=ALU.mult,
-            ),
-        ]
-
-        def advance(count):
-            for step in steps[:count]:
-                step()
-            for step in steps[:count]:
-                steps.remove(step)
-
-        turn(0)
-        evacuate(0)
-        square_rows(0)
-        turn(1)
-        evacuate(1)
-        quantise(0)
-        b_sq = wide("b_sq", N // P)
-        b_part = wide("b_part", 1)
-        stt(
-            out=b_sq[:], in0=b_cols[:], scalar=1.0, in1=b_cols[:], op0=ALU.mult, op1=ALU.mult,
-            accum_out=b_part[:],
-        )
-        turn(2)
-        evacuate(2)
-        square_rows(1)
-        quantise(1)
-        turn(3)
-        evacuate(3)
-        quantise(2)
-        b_tot = psum.tile([P, 1], F32, tag="bank0", name="b_tot")
-        nc.tensor.matmul(b_tot[:], lhsT=ones_f[:], rhs=b_part[:], start=True, stop=True)
-        turn(4)
-        evacuate(4)
-        nc.vector.tensor_copy(out=sums[:, X_BLOCKS : X_BLOCKS + 1], in_=b_tot[:])
-        square_rows(2)
-        quantise(3)
-        turn(5)
-        evacuate(5)
-        quantise(4)
-        b_psum = psum.tile([P, N], BF16, tag="bank1", name="b_psum")
-
-        def spread_bias(h):
-            cols = slice(BANK * h, BANK * (h + 1))
-            nc.tensor.matmul(b_psum[:, cols], lhsT=ones[:], rhs=b_row0[:, cols], start=True, stop=True)
-
-        spread_bias(0)
-        square_rows(3)
-        turn(6)
-        evacuate(6)
-        advance(1)
-        quantise(5)
-        turn(7)
-        evacuate(7)
-        spread_bias(1)
-        advance(1)
-        quantise(6)
-        advance(2)
-        turn(8)
-        evacuate(8)
-        quantise(7)
-        advance(3)
-        nc.scalar.copy(out=b_all[:], in_=b_psum[:])
-        turn(9)
-        evacuate(9)
-        quantise(8)
-        advance(3)
-        turn(10)
-        evacuate(10)
-        quantise(9)
-        advance(3)
-        turn(11)
-        evacuate(11)
-        for t in range(X_BLOCKS):
-            multiply(0, t)
-        quantise(10)
-        advance(2)
-        square_mx(0, 0)
-        quantise(11)
-        advance(1)
-        for t in range(X_BLOCKS):
-            multiply(1, t)
-        dot_mx(0, 1)
-        dot_mx(0, 0)
-        log_ratio = wide("log_ratio", X_BLOCKS)
-        nc.scalar.activation(out=log_ratio[:], in_=ratio[:], func=ACT.Ln)
-        b_tanh = wide("b_tanh", 1)
-        nc.scalar.activation(out=b_tanh[:], in_=g[3][:, X_BLOCKS : X_BLOCKS + 1], func=ACT.Tanh)
-        square_mx(0, 1)
-        dot_mx(1, 0)
-        square_mx(1, 0)
-        dot_mx(1, 1)
-        gain = wide("gain", X_BLOCKS)
-        stt(
-            out=gain[:], in0=log_ratio[:], scalar=0.5 * SEED, in1=y[3][:, 0:X_BLOCKS],
-            op0=ALU.mult, op1=ALU.mult,
-        )
-        square_mx(1, 1)
-        q_scale = wide("q_scale", 1)
-        nc.vector.tensor_scalar(
-            out=q_scale[:], in0=b_tanh[:], scalar1=y[3][:, X_BLOCKS : X_BLOCKS + 1], scalar2=SEED,
-            op0=ALU.mult, op1=ALU.mult,
-        )
-        q_twice = wide("q_twice", 1)
-        nc.vector.tensor_scalar_mul(out=q_twice[:], in0=q_scale[:], scalar1=2.0)
-        q_neg = wide("q_neg", 1)
-        nc.vector.tensor_scalar_mul(out=q_neg[:], in0=q_scale[:], scalar1=-1.0)
-        qq = wide("qq", 1)
-        nc.vector.tensor_scalar(
-            out=qq[:], in0=sums[:, X_BLOCKS : X_BLOCKS + 1], scalar1=q_scale[:, 0:1],
-            scalar2=q_scale[:, 0:1], op0=ALU.mult, op1=ALU.mult,
-        )
-        qq_plus_1 = wide("qq_plus_1", 1)
-        nc.vector.tensor_scalar_add(out=qq_plus_1[:], in0=qq[:], scalar1=1.0)
-        edge_scale = wide("edge_scale", 1)
-        nc.vector.tensor_scalar(
-            out=edge_scale[:], in0=qq[:], scalar1=0.5 / (MAXN * MAXN), scalar2=-0.5 / (MAXN * MAXN),
-            op0=ALU.mult, op1=ALU.add,
-        )
 
         s = wide("s", X_BLOCKS)
+        inv_s = wide("inv_s", X_BLOCKS)
         mxn = wide("mxn", X_BLOCKS)
         inv_mxn = wide("inv_mxn", X_BLOCKS)
         th = wide("th", X_BLOCKS)
         d = wide("d", X_BLOCKS)
         w = wide("w", X_BLOCKS)
-        v = wide("v", X_BLOCKS)
         t1 = wide("t1", X_BLOCKS)
         p2 = wide("p2", X_BLOCKS)
         den_1 = wide("den_1", X_BLOCKS)
@@ -332,18 +168,25 @@ def tile_directnodecomphyperbolicforecaster_pa_kernel(tc, v_init, W_vel, b_vel, 
         inv = wide("inv", X_BLOCKS)
         shrink_den = wide("shrink_den", X_BLOCKS)
         shrink = wide("shrink", X_BLOCKS)
-        ari = wide("ari", X_BLOCKS)
-        cbi = wide("cbi", X_BLOCKS)
+        f = wide("f", X_BLOCKS)
         coef_b = wide("coef_b", X_BLOCKS)
         coef_mx = wide("coef_mx", X_BLOCKS)
+        q_twice = wide("q_twice", 1)
+        q_neg = wide("q_neg", 1)
+        qq = wide("qq", 1)
+        qq_plus_1 = wide("qq_plus_1", 1)
+        edge_scale = wide("edge_scale", 1)
 
-        def sum_squares(c):
+        def norms_of_mx(c):
             for t in range(c.start, c.stop):
-                nc.vector.tensor_scalar(
+                nc.gpsimd.tensor_scalar(
                     out=s[:, t : t + 1], in0=mx_sq[:, 0, t : t + 1], scalar1=mx_sq[:, 1, t : t + 1],
                     scalar2=EPS, op0=ALU.add, op1=ALU.max,
                 )
-            nc.gpsimd.tensor_tensor(out=mxn[:, c], in0=s[:, c], in1=half[:], op=ALU.pow)
+            nc.gpsimd.tensor_tensor(out=mxn[:, c], in0=s[:, c], in1=half[:, c], op=ALU.pow)
+
+        def inverse_squares(c):
+            nc.vector.reciprocal(out=inv_s[:, c], in_=s[:, c])
 
         def tanhs(c):
             for t in range(c.start, c.stop):
@@ -351,38 +194,35 @@ def tile_directnodecomphyperbolicforecaster_pa_kernel(tc, v_init, W_vel, b_vel, 
                     out=th[:, t : t + 1], in_=mxn[:, t : t + 1], func=ACT.Tanh, scale=gain[:, t : t + 1]
                 )
 
-        def dots(c):
-            nc.vector.tensor_add(out=d[:, c], in0=mx_b[:, 0, c], in1=mx_b[:, 1, c])
-
-        def inverse_norms(c):
-            nc.vector.reciprocal(out=inv_mxn[:, c], in_=mxn[:, c])
-
         def weights(c):
+            nc.gpsimd.tensor_mul(out=inv_mxn[:, c], in0=mxn[:, c], in1=inv_s[:, c])
+            nc.gpsimd.tensor_add(out=d[:, c], in0=mx_b[:, 0, c], in1=mx_b[:, 1, c])
+            nc.gpsimd.tensor_mul(out=w[:, c], in0=d[:, c], in1=inv_mxn[:, c])
+
+        def coef_1(c):
+            nc.vector.tensor_mul(out=p2[:, c], in0=th[:, c], in1=th[:, c])
             stt(
-                out=w[:, c], in0=d[:, c], scalar=q_twice[:, 0:1], in1=inv_mxn[:, c], op0=ALU.mult,
+                out=t1[:, c], in0=w[:, c], scalar=q_twice[:, 0:1], in1=th[:, c], op0=ALU.mult,
+                op1=ALU.mult,
+            )
+            nc.gpsimd.tensor_mul(out=thi[:, c], in0=th[:, c], in1=inv_mxn[:, c])
+            nc.gpsimd.tensor_scalar(
+                out=edge[:, c], in0=p2[:, c], scalar1=1.0, scalar2=edge_scale[:, 0:1],
+                op0=ALU.subtract, op1=ALU.mult,
+            )
+            nc.gpsimd.tensor_scalar(
+                out=cbq[:, c], in0=p2[:, c], scalar1=1.0, scalar2=q_neg[:, 0:1], op0=ALU.subtract,
                 op1=ALU.mult,
             )
 
-        def coef_1(c):
-            stt(out=v[:, c], in0=th[:, c], scalar=qq[:, 0:1], in1=w[:, c], op0=ALU.mult, op1=ALU.add)
-            nc.vector.tensor_mul(out=t1[:, c], in0=th[:, c], in1=w[:, c])
-            nc.vector.tensor_mul(out=p2[:, c], in0=th[:, c], in1=th[:, c])
-
         def coef_2(c):
-            nc.vector.tensor_mul(out=den_1[:, c], in0=v[:, c], in1=th[:, c])
-            nc.vector.tensor_mul(out=thi[:, c], in0=th[:, c], in1=inv_mxn[:, c])
-            nc.vector.tensor_scalar(
-                out=cbq[:, c], in0=p2[:, c], scalar1=1.0, scalar2=q_neg[:, 0:1], op0=ALU.subtract,
-                op1=ALU.mult,
+            stt(
+                out=den_1[:, c], in0=p2[:, c], scalar=qq[:, 0:1], in1=t1[:, c], op0=ALU.mult, op1=ALU.add
             )
 
         def coef_3(c):
             nc.vector.tensor_scalar(
                 out=den[:, c], in0=den_1[:, c], scalar1=1.0, scalar2=EPS, op0=ALU.add, op1=ALU.max
-            )
-            nc.vector.tensor_scalar(
-                out=edge[:, c], in0=p2[:, c], scalar1=1.0, scalar2=edge_scale[:, 0:1],
-                op0=ALU.subtract, op1=ALU.mult,
             )
             stt(
                 out=ar[:, c], in0=t1[:, c], scalar=qq_plus_1[:, 0:1], in1=thi[:, c], op0=ALU.add,
@@ -398,15 +238,11 @@ def tile_directnodecomphyperbolicforecaster_pa_kernel(tc, v_init, W_vel, b_vel, 
 
         def coef_5(c):
             nc.vector.tensor_mul(out=shrink[:, c], in0=shrink_den[:, c], in1=inv[:, c])
-            nc.vector.tensor_mul(out=cbi[:, c], in0=cbq[:, c], in1=inv[:, c])
-            nc.vector.tensor_mul(out=ari[:, c], in0=ar[:, c], in1=inv[:, c])
 
         def coef_6(c):
-            for out_c, in_c in ((coef_b, cbi), (coef_mx, ari)):
-                stt(
-                    out=out_c[:, c], in0=shrink[:, c], scalar=1.0, in1=in_c[:, c], op0=ALU.min,
-                    op1=ALU.mult,
-                )
+            stt(out=f[:, c], in0=shrink[:, c], scalar=1.0, in1=inv[:, c], op0=ALU.min, op1=ALU.mult)
+            nc.vector.tensor_mul(out=coef_b[:, c], in0=cbq[:, c], in1=f[:, c])
+            nc.vector.tensor_mul(out=coef_mx[:, c], in0=ar[:, c], in1=f[:, c])
 
         b_term = [wide("b_term%d" % t, N) for t in range(X_BLOCKS)]
         result = [wide("result%d" % t, N) for t in range(X_BLOCKS)]
@@ -437,57 +273,184 @@ def tile_directnodecomphyperbolicforecaster_pa_kernel(tc, v_init, W_vel, b_vel, 
                 in1=b_term[t][:, cols], op0=ALU.mult, op1=ALU.add,
             )
 
-        def store(t):
-            nc.sync.dma_start(out=out[P * t : P * (t + 1), :], in_=result[t][:])
+        scaled = {}
 
-        first_pair, second_pair = slice(0, 2), slice(2, 4)
-        dot_mx(0, 3)
-        dots(first_pair)
-        square_mx(0, 2)
-        sum_squares(first_pair)
+        def scale_scalar(t, h):
+            scaled[(t, h)] = wide("scaled%d%d" % (t, h), BANK)
+            nc.scalar.activation(
+                out=scaled[(t, h)][:], in_=mx[(h, t)][:], func=ACT.Copy, scale=coef_mx[:, t : t + 1]
+            )
+
+        def finish_gpsimd(t, h):
+            cols = slice(BANK * h, BANK * (h + 1))
+            nc.gpsimd.tensor_add(out=result[t][:, cols], in0=scaled[(t, h)][:], in1=b_term[t][:, cols])
+
+        def store(t, h0, h1):
+            cols = slice(BANK * h0, BANK * h1)
+            nc.sync.dma_start(out=out[P * t : P * (t + 1), cols], in_=result[t][:, cols])
+
+        pair_a, pair_b = slice(0, 2), slice(2, 4)
+
+        turn(0)
+        evacuate(0)
+        square_rows(0)
+        turn(1)
+        evacuate(1)
+        quantise(0)
+        b_sq = wide("b_sq", N // P)
+        b_part = wide("b_part", 1)
+        stt(
+            out=b_sq[:], in0=b_cols[:], scalar=1.0, in1=b_cols[:], op0=ALU.mult, op1=ALU.mult,
+            accum_out=b_part[:],
+        )
+        square_rows(1)
+        turn(2)
+        evacuate(2)
+        quantise(1)
+        b_tot = psum.tile([P, 1], F32, tag="bank0", name="b_tot")
+        nc.tensor.matmul(b_tot[:], lhsT=ones_f[:], rhs=b_part[:], start=True, stop=True)
+        turn(3)
+        evacuate(3)
+        quantise(2)
+        nc.vector.tensor_copy(out=sums[:, X_BLOCKS : X_BLOCKS + 1], in_=b_tot[:])
+        square_rows(2)
+        turn(4)
+        evacuate(4)
+        quantise(3)
+        turn(5)
+        evacuate(5)
+        quantise(4)
+        square_rows(3)
+        sums_c = wide("sums_c", X_BLOCKS + 1)
+        norms = wide("norms", X_BLOCKS + 1)
+        inv_norms = wide("inv_norms", X_BLOCKS + 1)
+        clipped = wide("clipped", X_BLOCKS)
+        nc.gpsimd.tensor_scalar_max(out=sums_c[:], in0=sums[:], scalar1=EPS)
+        nc.gpsimd.tensor_tensor(out=norms[:], in0=sums_c[:], in1=half[:], op=ALU.pow)
+        nc.gpsimd.tensor_scalar_min(out=clipped[:], in0=norms[:, 0:X_BLOCKS], scalar1=1.0 - 1e-7)
+        nc.gpsimd.tensor_tensor(out=inv_norms[:], in0=sums_c[:], in1=neg_half[:], op=ALU.pow)
+        turn(6)
+        evacuate(6)
+        quantise(5)
+        turn(7)
+        evacuate(7)
+        quantise(6)
+        turn(8)
+        evacuate(8)
+        quantise(7)
+        turn(9)
+        evacuate(9)
+        quantise(8)
+        turn(10)
+        evacuate(10)
+        quantise(9)
+        turn(11)
+        evacuate(11)
+        b_psum = psum.tile([P, N], BF16, tag="bank3", name="b_psum")
+
+        def spread_bias(h):
+            cols = slice(BANK * h, BANK * (h + 1))
+            nc.tensor.matmul(b_psum[:, cols], lhsT=ones[:], rhs=b_row0[:, cols], start=True, stop=True)
+
+        spread_bias(0)
+        spread_bias(1)
+        nc.scalar.copy(out=b_all[:], in_=b_psum[:])
+        quantise(10)
+        multiply(0, 1)
+        quantise(11)
+        multiply(0, 0)
+        multiply(1, 0)
+        multiply(0, 2)
+        multiply(1, 1)
+        square_mx(0, 0)
+        log_plus = wide("log_plus", X_BLOCKS)
+        nc.scalar.activation(out=log_plus[:], in_=clipped[:], func=ACT.Ln, bias=ones_f[:, 0:1], scale=1.0)
+        log_minus = wide("log_minus", X_BLOCKS)
+        nc.scalar.activation(
+            out=log_minus[:], in_=clipped[:], func=ACT.Ln, bias=ones_f[:, 0:1], scale=-1.0
+        )
+        twice_artanh = wide("twice_artanh", X_BLOCKS)
+        nc.gpsimd.tensor_sub(out=twice_artanh[:], in0=log_plus[:], in1=log_minus[:])
+        gain_2 = wide("gain_2", X_BLOCKS)
+        nc.gpsimd.tensor_mul(out=gain_2[:], in0=twice_artanh[:], in1=inv_norms[:, 0:X_BLOCKS])
+        gain = wide("gain", X_BLOCKS)
+        nc.gpsimd.tensor_scalar(
+            out=gain[:], in0=gain_2[:], scalar1=0.5, scalar2=0.0, op0=ALU.mult, op1=ALU.add
+        )
+        multiply(1, 2)
+        multiply(1, 3)
+        multiply(0, 3)
+        dot_mx(0, 1)
+        dot_mx(0, 0)
+        square_mx(0, 1)
         dot_mx(0, 2)
-        square_mx(0, 3)
-        inverse_norms(first_pair)
-        weights(first_pair)
-        tanhs(first_pair)
-        dot_mx(1, 3)
-        square_mx(1, 2)
-        coef_1(first_pair)
-        coef_2(first_pair)
-        coef_3(first_pair)
-        square_mx(1, 3)
-        coef_4(first_pair)
-        coef_5(first_pair)
-        coef_6(first_pair)
-        bias(0, 0)
-        bias(0, 1)
+        square_mx(1, 0)
+        dot_mx(1, 0)
+        square_mx(1, 1)
+        b_tanh = wide("b_tanh", 1)
+        nc.scalar.activation(out=b_tanh[:], in_=norms[:, X_BLOCKS : X_BLOCKS + 1], func=ACT.Tanh)
+        norms_of_mx(pair_a)
+        dot_mx(1, 1)
+        inverse_squares(pair_a)
+        weights(pair_a)
+        tanhs(pair_a)
         dot_mx(1, 2)
-        dots(second_pair)
-        sum_squares(second_pair)
-        bias_gpsimd(1, 0)
+        dot_mx(1, 3)
+        inv_bn = inv_norms[:, X_BLOCKS : X_BLOCKS + 1]
+        nc.vector.tensor_scalar(
+            out=q_twice[:], in0=b_tanh[:], scalar1=inv_bn, scalar2=2.0, op0=ALU.mult, op1=ALU.mult
+        )
+        nc.vector.tensor_scalar(
+            out=q_neg[:], in0=b_tanh[:], scalar1=inv_bn, scalar2=-1.0, op0=ALU.mult, op1=ALU.mult
+        )
+        nc.vector.tensor_mul(out=qq[:], in0=b_tanh[:], in1=b_tanh[:])
+        nc.vector.tensor_scalar(
+            out=qq_plus_1[:], in0=b_tanh[:], scalar1=b_tanh[:, 0:1], scalar2=1.0, op0=ALU.mult, op1=ALU.add
+        )
+        nc.vector.tensor_scalar(
+            out=edge_scale[:], in0=qq[:], scalar1=0.5 / (MAXN * MAXN), scalar2=-0.5 / (MAXN * MAXN),
+            op0=ALU.mult, op1=ALU.add,
+        )
+        square_mx(0, 2)
+        square_mx(0, 3)
+        coef_1(pair_a)
+        coef_2(pair_a)
+        coef_3(pair_a)
+        square_mx(1, 2)
+        square_mx(1, 3)
+        dot_mx(0, 3)
+        coef_4(pair_a)
+        coef_5(pair_a)
+        norms_of_mx(pair_b)
+        inverse_squares(pair_b)
+        coef_6(pair_a)
+        bias(0, 1)
+        tanhs(pair_b)
+        bias_vector(0, 0)
+        bias(1, 0)
+        weights(pair_b)
         finish(0, 0)
-        tanhs(second_pair)
         bias(1, 1)
-        inverse_norms(second_pair)
         finish(0, 1)
-        store(0)
-        weights(second_pair)
+        store(0, 0, 2)
+        coef_1(pair_b)
+        coef_2(pair_b)
         finish(1, 0)
-        coef_1(second_pair)
-        coef_2(second_pair)
-        coef_3(second_pair)
+        coef_3(pair_b)
+        coef_4(pair_b)
         finish(1, 1)
-        store(1)
-        coef_4(second_pair)
-        coef_5(second_pair)
-        coef_6(second_pair)
+        store(1, 0, 2)
+        coef_5(pair_b)
+        coef_6(pair_b)
         bias_vector(2, 0)
         bias(2, 1)
+        scale_scalar(3, 1)
         bias(3, 0)
         bias_gpsimd(3, 1)
         finish(2, 0)
         finish(2, 1)
-        store(2)
+        store(2, 0, 2)
         finish(3, 0)
-        finish(3, 1)
-        store(3)
+        store(3, 0, 1)
+        finish_gpsimd(3, 1)
+        store(3, 1, 2)

@@ -1,3 +1,4 @@
+import math
 from contextlib import ExitStack
 
 import concourse.mybir as mybir
@@ -62,8 +63,6 @@ def tile_directnodecomphyperbolicforecaster_pa_kernel(tc, v_init, W_vel, b_vel, 
         make_identity(nc, ident[:])
         half = wide("half", X_BLOCKS + 1)
         nc.gpsimd.memset(half[:], 0.5)
-        neg_half = wide("neg_half", X_BLOCKS + 1)
-        nc.gpsimd.memset(neg_half[:], -0.5)
         ones = keep.tile([P, P], BF16, name="ones")
         nc.vector.memset(ones[:], 1.0)
         ones_f = wide("ones_f", P)
@@ -87,9 +86,9 @@ def tile_directnodecomphyperbolicforecaster_pa_kernel(tc, v_init, W_vel, b_vel, 
                     nc.tensor.transpose(f[:, g, u, :], words[:, start : start + P], ident[:])
             flipped[i] = f
 
-        def evacuate(i):
+        def evacuate(i, copy):
             t = keep.tile([P, PASSES * 4 * P], BF16, align_bytes=64, name="grouped%d" % i)
-            nc.scalar.copy(
+            copy(
                 out=t[:].bitcast(F32).rearrange("p (g c u) -> p g c u", g=PASSES, u=2),
                 in_=flipped[i][:].rearrange("p g u c -> p g c u"),
             )
@@ -114,6 +113,12 @@ def tile_directnodecomphyperbolicforecaster_pa_kernel(tc, v_init, W_vel, b_vel, 
             nc.vector.scalar_tensor_tensor(
                 out=sq[:], in0=blocks[i][:], scalar=1.0, in1=blocks[i][:], op0=ALU.mult,
                 op1=ALU.mult, accum_out=sums[:, i : i + 1],
+            )
+
+        def square_rows_scalar(i):
+            sq = keep.tile([P, K], BF16, name="x_sq%d" % i)
+            nc.scalar.activation(
+                out=sq[:], in_=blocks[i][:], func=ACT.Square, accum_out=sums[:, i : i + 1]
             )
 
         mx = {}
@@ -150,99 +155,189 @@ def tile_directnodecomphyperbolicforecaster_pa_kernel(tc, v_init, W_vel, b_vel, 
 
         stt = nc.vector.scalar_tensor_tensor
 
+        b_sq = wide("b_sq", N // P)
+        b_part = wide("b_part", 1)
+        stt(
+            out=b_sq[:], in0=b_cols[:], scalar=1.0, in1=b_cols[:], op0=ALU.mult, op1=ALU.mult,
+            accum_out=b_part[:],
+        )
+        turn(0)
+        evacuate(0, nc.scalar.copy)
+        square_rows(0)
+        turn(1)
+        evacuate(1, nc.scalar.copy)
+        square_rows(1)
+        turn(2)
+        b_tot = psum.tile([P, 1], F32, tag="bank7", name="b_tot")
+        nc.tensor.matmul(b_tot[:], lhsT=ones_f[:], rhs=b_part[:], start=True, stop=True)
+        square_rows_scalar(3)
+        nc.vector.tensor_copy(out=sums[:, X_BLOCKS : X_BLOCKS + 1], in_=b_tot[:])
+        square_rows(2)
+        turn(3)
+        evacuate(2, nc.scalar.copy)
+        evacuate(3, nc.scalar.copy)
+        turn(4)
+        evacuate(4, nc.scalar.copy)
+        b_psum = psum.tile([P, N], BF16, tag="bank0", name="b_psum")
+
+        def spread_bias(h):
+            cols = slice(BANK * h, BANK * (h + 1))
+            nc.tensor.matmul(b_psum[:, cols], lhsT=ones[:], rhs=b_row0[:, cols], start=True, stop=True)
+
+        spread_bias(0)
+        turn(5)
+        sums_c = wide("sums_c", X_BLOCKS + 1)
+        norms = wide("norms", X_BLOCKS + 1)
+        inv_norms = wide("inv_norms", X_BLOCKS + 1)
+        clipped = wide("clipped", X_BLOCKS)
+        nc.vector.tensor_scalar_max(out=sums_c[:], in0=sums[:], scalar1=EPS)
+        nc.gpsimd.tensor_tensor(out=norms[:], in0=sums_c[:], in1=half[:], op=ALU.pow)
+        quantise(0)
+        evacuate(5, nc.vector.tensor_copy)
+        turn(6)
+        evacuate(6, nc.scalar.copy)
+        quantise(1)
+        spread_bias(1)
+        turn(7)
+        evacuate(7, nc.scalar.copy)
+        for i in range(2, 7):
+            quantise(i)
+        turn(8)
+        evacuate(8, nc.scalar.copy)
+        turn(9)
+        evacuate(9, nc.scalar.copy)
+        quantise(7)
+        nc.vector.tensor_scalar_min(out=clipped[:], in0=norms[:, 0:X_BLOCKS], scalar1=1.0 - 1e-7)
+        turn(10)
+        evacuate(10, nc.scalar.copy)
+        quantise(8)
+        nc.vector.reciprocal(out=inv_norms[:], in_=norms[:])
+        nc.vector.tensor_copy(out=b_all[:], in_=b_psum[:])
+        multiply(0, 1)
+        turn(11)
+        square_mx(0, 1)
+        evacuate(11, nc.scalar.copy)
+        multiply(0, 2)
+        quantise(9)
+        quantise(10)
+        multiply(0, 0)
+        multiply(0, 3)
+        dot_mx(0, 1)
+        quantise(11)
+        log_plus = wide("log_plus", X_BLOCKS)
+        nc.scalar.activation(out=log_plus[:], in_=clipped[:], func=ACT.Ln, bias=ones_f[:, 0:1], scale=1.0)
+        log_minus = wide("log_minus", X_BLOCKS)
+        nc.scalar.activation(
+            out=log_minus[:], in_=clipped[:], func=ACT.Ln, bias=ones_f[:, 0:1], scale=-1.0
+        )
+        square_mx(0, 2)
+        dot_mx(0, 0)
+        multiply(1, 1)
+        multiply(1, 0)
+        multiply(1, 2)
+        multiply(1, 3)
+        square_mx(0, 3)
+        dot_mx(0, 2)
+        twice_artanh = wide("twice_artanh", X_BLOCKS)
+        nc.vector.tensor_sub(out=twice_artanh[:], in0=log_plus[:], in1=log_minus[:])
+        gain = wide("gain", X_BLOCKS)
+        stt(
+            out=gain[:], in0=twice_artanh[:], scalar=0.5, in1=inv_norms[:, 0:X_BLOCKS], op0=ALU.mult,
+            op1=ALU.mult,
+        )
         s = wide("s", X_BLOCKS)
-        inv_s = wide("inv_s", X_BLOCKS)
         mxn = wide("mxn", X_BLOCKS)
-        inv_mxn = wide("inv_mxn", X_BLOCKS)
-        th = wide("th", X_BLOCKS)
-        d = wide("d", X_BLOCKS)
-        w = wide("w", X_BLOCKS)
-        t1 = wide("t1", X_BLOCKS)
-        p2 = wide("p2", X_BLOCKS)
-        den_1 = wide("den_1", X_BLOCKS)
-        thi = wide("thi", X_BLOCKS)
-        cbq = wide("cbq", X_BLOCKS)
-        den = wide("den", X_BLOCKS)
-        edge = wide("edge", X_BLOCKS)
-        ar = wide("ar", X_BLOCKS)
-        inv = wide("inv", X_BLOCKS)
-        shrink_den = wide("shrink_den", X_BLOCKS)
-        shrink = wide("shrink", X_BLOCKS)
-        f = wide("f", X_BLOCKS)
-        coef_b = wide("coef_b", X_BLOCKS)
-        coef_mx = wide("coef_mx", X_BLOCKS)
-        q_twice = wide("q_twice", 1)
-        q_neg = wide("q_neg", 1)
-        qq = wide("qq", 1)
-        qq_plus_1 = wide("qq_plus_1", 1)
-        edge_scale = wide("edge_scale", 1)
 
         def norms_of_mx(c):
-            for t in range(c.start, c.stop):
-                nc.gpsimd.tensor_scalar(
-                    out=s[:, t : t + 1], in0=mx_sq[:, 0, t : t + 1], scalar1=mx_sq[:, 1, t : t + 1],
-                    scalar2=EPS, op0=ALU.add, op1=ALU.max,
-                )
+            nc.vector.tensor_add(out=s[:, c], in0=mx_sq[:, 0, c], in1=mx_sq[:, 1, c])
             nc.gpsimd.tensor_tensor(out=mxn[:, c], in0=s[:, c], in1=half[:, c], op=ALU.pow)
 
-        def inverse_squares(c):
-            nc.vector.reciprocal(out=inv_s[:, c], in_=s[:, c])
-
-        def tanhs(c):
-            for t in range(c.start, c.stop):
-                nc.scalar.activation(
-                    out=th[:, t : t + 1], in_=mxn[:, t : t + 1], func=ACT.Tanh, scale=gain[:, t : t + 1]
-                )
-
-        def weights(c):
-            nc.gpsimd.tensor_mul(out=inv_mxn[:, c], in0=mxn[:, c], in1=inv_s[:, c])
-            nc.gpsimd.tensor_add(out=d[:, c], in0=mx_b[:, 0, c], in1=mx_b[:, 1, c])
-            nc.gpsimd.tensor_mul(out=w[:, c], in0=d[:, c], in1=inv_mxn[:, c])
-
-        def coef_1(c):
-            nc.vector.tensor_mul(out=p2[:, c], in0=th[:, c], in1=th[:, c])
-            stt(
-                out=t1[:, c], in0=w[:, c], scalar=q_twice[:, 0:1], in1=th[:, c], op0=ALU.mult,
-                op1=ALU.mult,
+        square_mx(0, 0)
+        dot_mx(0, 3)
+        square_mx(1, 1)
+        square_mx(1, 0)
+        dot_mx(1, 1)
+        square_mx(1, 2)
+        norms_of_mx(slice(0, 2))
+        dot_mx(1, 0)
+        square_mx(1, 3)
+        dot_mx(1, 2)
+        norms_of_mx(slice(2, 4))
+        dot_mx(1, 3)
+        d = wide("d", X_BLOCKS)
+        nc.vector.tensor_add(out=d[:], in0=mx_b[:, 0, :], in1=mx_b[:, 1, :])
+        mxn_c = wide("mxn_c", X_BLOCKS)
+        nc.vector.tensor_scalar_max(out=mxn_c[:], in0=mxn[:], scalar1=math.sqrt(EPS))
+        inv_mxn = wide("inv_mxn", X_BLOCKS)
+        nc.vector.reciprocal(out=inv_mxn[:], in_=mxn_c[:])
+        w = wide("w", X_BLOCKS)
+        nc.vector.tensor_mul(out=w[:], in0=d[:], in1=inv_mxn[:])
+        b_tanh = wide("b_tanh", 1)
+        nc.scalar.activation(out=b_tanh[:], in_=norms[:, X_BLOCKS : X_BLOCKS + 1], func=ACT.Tanh)
+        th = wide("th", X_BLOCKS)
+        for t in range(X_BLOCKS):
+            nc.scalar.activation(
+                out=th[:, t : t + 1], in_=mxn[:, t : t + 1], func=ACT.Tanh, scale=gain[:, t : t + 1]
             )
-            nc.gpsimd.tensor_mul(out=thi[:, c], in0=th[:, c], in1=inv_mxn[:, c])
-            nc.gpsimd.tensor_scalar(
-                out=edge[:, c], in0=p2[:, c], scalar1=1.0, scalar2=edge_scale[:, 0:1],
-                op0=ALU.subtract, op1=ALU.mult,
-            )
-            nc.gpsimd.tensor_scalar(
-                out=cbq[:, c], in0=p2[:, c], scalar1=1.0, scalar2=q_neg[:, 0:1], op0=ALU.subtract,
-                op1=ALU.mult,
-            )
-
-        def coef_2(c):
-            stt(
-                out=den_1[:, c], in0=p2[:, c], scalar=qq[:, 0:1], in1=t1[:, c], op0=ALU.mult, op1=ALU.add
-            )
-
-        def coef_3(c):
-            nc.vector.tensor_scalar(
-                out=den[:, c], in0=den_1[:, c], scalar1=1.0, scalar2=EPS, op0=ALU.add, op1=ALU.max
-            )
-            stt(
-                out=ar[:, c], in0=t1[:, c], scalar=qq_plus_1[:, 0:1], in1=thi[:, c], op0=ALU.add,
-                op1=ALU.mult,
-            )
-
-        def coef_4(c):
-            nc.vector.reciprocal(out=inv[:, c], in_=den[:, c])
-            stt(
-                out=shrink_den[:, c], in0=den[:, c], scalar=EDGE, in1=edge[:, c], op0=ALU.mult,
-                op1=ALU.add,
-            )
-
-        def coef_5(c):
-            nc.vector.tensor_mul(out=shrink[:, c], in0=shrink_den[:, c], in1=inv[:, c])
-
-        def coef_6(c):
-            stt(out=f[:, c], in0=shrink[:, c], scalar=1.0, in1=inv[:, c], op0=ALU.min, op1=ALU.mult)
-            nc.vector.tensor_mul(out=coef_b[:, c], in0=cbq[:, c], in1=f[:, c])
-            nc.vector.tensor_mul(out=coef_mx[:, c], in0=ar[:, c], in1=f[:, c])
+        inv_bn = inv_norms[:, X_BLOCKS : X_BLOCKS + 1]
+        q_twice = wide("q_twice", 1)
+        nc.vector.tensor_scalar(
+            out=q_twice[:], in0=b_tanh[:], scalar1=inv_bn, scalar2=2.0, op0=ALU.mult, op1=ALU.mult
+        )
+        qq = wide("qq", 1)
+        nc.vector.tensor_mul(out=qq[:], in0=b_tanh[:], in1=b_tanh[:])
+        q_scale = wide("q_scale", 1)
+        nc.vector.tensor_mul(out=q_scale[:], in0=b_tanh[:], in1=inv_bn)
+        qq_plus_1 = wide("qq_plus_1", 1)
+        nc.vector.tensor_scalar(
+            out=qq_plus_1[:], in0=b_tanh[:], scalar1=b_tanh[:, 0:1], scalar2=1.0, op0=ALU.mult, op1=ALU.add
+        )
+        t1 = wide("t1", X_BLOCKS)
+        stt(out=t1[:], in0=w[:], scalar=q_twice[:, 0:1], in1=th[:], op0=ALU.mult, op1=ALU.mult)
+        p2 = wide("p2", X_BLOCKS)
+        nc.vector.tensor_mul(out=p2[:], in0=th[:], in1=th[:])
+        edge_bias = wide("edge_bias", 1)
+        nc.vector.tensor_scalar(
+            out=edge_bias[:], in0=qq[:], scalar1=-0.5 / (MAXN * MAXN), scalar2=0.5 / (MAXN * MAXN),
+            op0=ALU.mult, op1=ALU.add,
+        )
+        edge_scale = wide("edge_scale", 1)
+        nc.vector.tensor_scalar(
+            out=edge_scale[:], in0=qq[:], scalar1=0.5 / (MAXN * MAXN), scalar2=-0.5 / (MAXN * MAXN),
+            op0=ALU.mult, op1=ALU.add,
+        )
+        den_1 = wide("den_1", X_BLOCKS)
+        stt(out=den_1[:], in0=p2[:], scalar=qq[:, 0:1], in1=t1[:], op0=ALU.mult, op1=ALU.add)
+        edge = wide("edge", X_BLOCKS)
+        nc.scalar.activation(
+            out=edge[:], in_=p2[:], func=ACT.Identity, scale=edge_scale[:, 0:1], bias=edge_bias[:, 0:1]
+        )
+        one_minus_p2 = wide("one_minus_p2", X_BLOCKS)
+        nc.scalar.activation(
+            out=one_minus_p2[:], in_=p2[:], func=ACT.Identity, scale=-1.0, bias=ones_f[:, 0:1]
+        )
+        thi = wide("thi", X_BLOCKS)
+        nc.vector.tensor_mul(out=thi[:], in0=th[:], in1=inv_mxn[:])
+        den = wide("den", X_BLOCKS)
+        nc.vector.tensor_scalar(
+            out=den[:], in0=den_1[:], scalar1=1.0, scalar2=EPS, op0=ALU.add, op1=ALU.max
+        )
+        ar = wide("ar", X_BLOCKS)
+        stt(out=ar[:], in0=t1[:], scalar=qq_plus_1[:, 0:1], in1=thi[:], op0=ALU.add, op1=ALU.mult)
+        inv = wide("inv", X_BLOCKS)
+        nc.vector.reciprocal(out=inv[:], in_=den[:])
+        shrink_den = wide("shrink_den", X_BLOCKS)
+        stt(out=shrink_den[:], in0=den[:], scalar=EDGE, in1=edge[:], op0=ALU.mult, op1=ALU.add)
+        shrink = wide("shrink", X_BLOCKS)
+        nc.vector.tensor_mul(out=shrink[:], in0=shrink_den[:], in1=inv[:])
+        cbi = wide("cbi", X_BLOCKS)
+        stt(out=cbi[:], in0=one_minus_p2[:], scalar=q_scale[:, 0:1], in1=inv[:], op0=ALU.mult, op1=ALU.mult)
+        ari = wide("ari", X_BLOCKS)
+        nc.vector.tensor_mul(out=ari[:], in0=ar[:], in1=inv[:])
+        coef_b = wide("coef_b", X_BLOCKS)
+        stt(out=coef_b[:], in0=shrink[:], scalar=1.0, in1=cbi[:], op0=ALU.min, op1=ALU.mult)
+        coef_mx = wide("coef_mx", X_BLOCKS)
+        stt(out=coef_mx[:], in0=shrink[:], scalar=1.0, in1=ari[:], op0=ALU.min, op1=ALU.mult)
 
         b_term = [wide("b_term%d" % t, N) for t in range(X_BLOCKS)]
         result = [wide("result%d" % t, N) for t in range(X_BLOCKS)]
@@ -289,168 +384,26 @@ def tile_directnodecomphyperbolicforecaster_pa_kernel(tc, v_init, W_vel, b_vel, 
             cols = slice(BANK * h0, BANK * h1)
             nc.sync.dma_start(out=out[P * t : P * (t + 1), cols], in_=result[t][:, cols])
 
-        pair_a, pair_b = slice(0, 2), slice(2, 4)
-
-        turn(0)
-        evacuate(0)
-        square_rows(0)
-        turn(1)
-        evacuate(1)
-        quantise(0)
-        b_sq = wide("b_sq", N // P)
-        b_part = wide("b_part", 1)
-        stt(
-            out=b_sq[:], in0=b_cols[:], scalar=1.0, in1=b_cols[:], op0=ALU.mult, op1=ALU.mult,
-            accum_out=b_part[:],
-        )
-        square_rows(1)
-        turn(2)
-        evacuate(2)
-        quantise(1)
-        b_tot = psum.tile([P, 1], F32, tag="bank0", name="b_tot")
-        nc.tensor.matmul(b_tot[:], lhsT=ones_f[:], rhs=b_part[:], start=True, stop=True)
-        turn(3)
-        evacuate(3)
-        quantise(2)
-        nc.vector.tensor_copy(out=sums[:, X_BLOCKS : X_BLOCKS + 1], in_=b_tot[:])
-        square_rows(2)
-        turn(4)
-        evacuate(4)
-        quantise(3)
-        turn(5)
-        evacuate(5)
-        quantise(4)
-        square_rows(3)
-        sums_c = wide("sums_c", X_BLOCKS + 1)
-        norms = wide("norms", X_BLOCKS + 1)
-        inv_norms = wide("inv_norms", X_BLOCKS + 1)
-        clipped = wide("clipped", X_BLOCKS)
-        nc.gpsimd.tensor_scalar_max(out=sums_c[:], in0=sums[:], scalar1=EPS)
-        nc.gpsimd.tensor_tensor(out=norms[:], in0=sums_c[:], in1=half[:], op=ALU.pow)
-        nc.gpsimd.tensor_scalar_min(out=clipped[:], in0=norms[:, 0:X_BLOCKS], scalar1=1.0 - 1e-7)
-        nc.gpsimd.tensor_tensor(out=inv_norms[:], in0=sums_c[:], in1=neg_half[:], op=ALU.pow)
-        turn(6)
-        evacuate(6)
-        quantise(5)
-        turn(7)
-        evacuate(7)
-        quantise(6)
-        turn(8)
-        evacuate(8)
-        quantise(7)
-        turn(9)
-        evacuate(9)
-        quantise(8)
-        turn(10)
-        evacuate(10)
-        quantise(9)
-        turn(11)
-        evacuate(11)
-        b_psum = psum.tile([P, N], BF16, tag="bank3", name="b_psum")
-
-        def spread_bias(h):
-            cols = slice(BANK * h, BANK * (h + 1))
-            nc.tensor.matmul(b_psum[:, cols], lhsT=ones[:], rhs=b_row0[:, cols], start=True, stop=True)
-
-        spread_bias(0)
-        spread_bias(1)
-        nc.scalar.copy(out=b_all[:], in_=b_psum[:])
-        quantise(10)
-        multiply(0, 1)
-        quantise(11)
-        multiply(0, 0)
-        multiply(1, 0)
-        multiply(0, 2)
-        multiply(1, 1)
-        square_mx(0, 0)
-        log_plus = wide("log_plus", X_BLOCKS)
-        nc.scalar.activation(out=log_plus[:], in_=clipped[:], func=ACT.Ln, bias=ones_f[:, 0:1], scale=1.0)
-        log_minus = wide("log_minus", X_BLOCKS)
-        nc.scalar.activation(
-            out=log_minus[:], in_=clipped[:], func=ACT.Ln, bias=ones_f[:, 0:1], scale=-1.0
-        )
-        twice_artanh = wide("twice_artanh", X_BLOCKS)
-        nc.gpsimd.tensor_sub(out=twice_artanh[:], in0=log_plus[:], in1=log_minus[:])
-        gain_2 = wide("gain_2", X_BLOCKS)
-        nc.gpsimd.tensor_mul(out=gain_2[:], in0=twice_artanh[:], in1=inv_norms[:, 0:X_BLOCKS])
-        gain = wide("gain", X_BLOCKS)
-        nc.gpsimd.tensor_scalar(
-            out=gain[:], in0=gain_2[:], scalar1=0.5, scalar2=0.0, op0=ALU.mult, op1=ALU.add
-        )
-        multiply(1, 2)
-        multiply(1, 3)
-        multiply(0, 3)
-        dot_mx(0, 1)
-        dot_mx(0, 0)
-        square_mx(0, 1)
-        dot_mx(0, 2)
-        square_mx(1, 0)
-        dot_mx(1, 0)
-        square_mx(1, 1)
-        b_tanh = wide("b_tanh", 1)
-        nc.scalar.activation(out=b_tanh[:], in_=norms[:, X_BLOCKS : X_BLOCKS + 1], func=ACT.Tanh)
-        norms_of_mx(pair_a)
-        dot_mx(1, 1)
-        inverse_squares(pair_a)
-        weights(pair_a)
-        tanhs(pair_a)
-        dot_mx(1, 2)
-        dot_mx(1, 3)
-        inv_bn = inv_norms[:, X_BLOCKS : X_BLOCKS + 1]
-        nc.vector.tensor_scalar(
-            out=q_twice[:], in0=b_tanh[:], scalar1=inv_bn, scalar2=2.0, op0=ALU.mult, op1=ALU.mult
-        )
-        nc.vector.tensor_scalar(
-            out=q_neg[:], in0=b_tanh[:], scalar1=inv_bn, scalar2=-1.0, op0=ALU.mult, op1=ALU.mult
-        )
-        nc.vector.tensor_mul(out=qq[:], in0=b_tanh[:], in1=b_tanh[:])
-        nc.vector.tensor_scalar(
-            out=qq_plus_1[:], in0=b_tanh[:], scalar1=b_tanh[:, 0:1], scalar2=1.0, op0=ALU.mult, op1=ALU.add
-        )
-        nc.vector.tensor_scalar(
-            out=edge_scale[:], in0=qq[:], scalar1=0.5 / (MAXN * MAXN), scalar2=-0.5 / (MAXN * MAXN),
-            op0=ALU.mult, op1=ALU.add,
-        )
-        square_mx(0, 2)
-        square_mx(0, 3)
-        coef_1(pair_a)
-        coef_2(pair_a)
-        coef_3(pair_a)
-        square_mx(1, 2)
-        square_mx(1, 3)
-        dot_mx(0, 3)
-        coef_4(pair_a)
-        coef_5(pair_a)
-        norms_of_mx(pair_b)
-        inverse_squares(pair_b)
-        coef_6(pair_a)
-        bias(0, 1)
-        tanhs(pair_b)
         bias_vector(0, 0)
+        bias(0, 1)
+        bias_gpsimd(1, 1)
+        scale_scalar(1, 1)
         bias(1, 0)
-        weights(pair_b)
         finish(0, 0)
-        bias(1, 1)
         finish(0, 1)
         store(0, 0, 2)
-        coef_1(pair_b)
-        coef_2(pair_b)
-        finish(1, 0)
-        coef_3(pair_b)
-        coef_4(pair_b)
-        finish(1, 1)
-        store(1, 0, 2)
-        coef_5(pair_b)
-        coef_6(pair_b)
-        bias_vector(2, 0)
-        bias(2, 1)
-        scale_scalar(3, 1)
-        bias(3, 0)
+        bias(2, 0)
+        finish_gpsimd(1, 1)
         bias_gpsimd(3, 1)
+        scale_scalar(3, 1)
+        finish(1, 0)
+        store(1, 0, 2)
+        bias(2, 1)
+        bias_vector(3, 0)
         finish(2, 0)
-        finish(2, 1)
-        store(2, 0, 2)
         finish(3, 0)
         store(3, 0, 1)
+        finish(2, 1)
+        store(2, 0, 2)
         finish_gpsimd(3, 1)
         store(3, 1, 2)

@@ -86,9 +86,9 @@ def tile_directnodecomphyperbolicforecaster_pa_kernel(tc, v_init, W_vel, b_vel, 
                     nc.tensor.transpose(f[:, g, u, :], words[:, start : start + P], ident[:])
             flipped[i] = f
 
-        def evacuate(i, copy):
+        def evacuate(i):
             t = keep.tile([P, PASSES * 4 * P], BF16, align_bytes=64, name="grouped%d" % i)
-            copy(
+            nc.scalar.copy(
                 out=t[:].bitcast(F32).rearrange("p (g c u) -> p g c u", g=PASSES, u=2),
                 in_=flipped[i][:].rearrange("p g u c -> p g c u"),
             )
@@ -162,10 +162,10 @@ def tile_directnodecomphyperbolicforecaster_pa_kernel(tc, v_init, W_vel, b_vel, 
             accum_out=b_part[:],
         )
         turn(0)
-        evacuate(0, nc.scalar.copy)
+        evacuate(0)
         square_rows(0)
         turn(1)
-        evacuate(1, nc.scalar.copy)
+        evacuate(1)
         square_rows(1)
         turn(2)
         b_tot = psum.tile([P, 1], F32, tag="bank7", name="b_tot")
@@ -174,10 +174,10 @@ def tile_directnodecomphyperbolicforecaster_pa_kernel(tc, v_init, W_vel, b_vel, 
         nc.vector.tensor_copy(out=sums[:, X_BLOCKS : X_BLOCKS + 1], in_=b_tot[:])
         square_rows(2)
         turn(3)
-        evacuate(2, nc.scalar.copy)
-        evacuate(3, nc.scalar.copy)
+        evacuate(2)
+        evacuate(3)
         turn(4)
-        evacuate(4, nc.scalar.copy)
+        evacuate(4)
         b_psum = psum.tile([P, N], BF16, tag="bank0", name="b_psum")
 
         def spread_bias(h):
@@ -193,30 +193,30 @@ def tile_directnodecomphyperbolicforecaster_pa_kernel(tc, v_init, W_vel, b_vel, 
         nc.vector.tensor_scalar_max(out=sums_c[:], in0=sums[:], scalar1=EPS)
         nc.gpsimd.tensor_tensor(out=norms[:], in0=sums_c[:], in1=half[:], op=ALU.pow)
         quantise(0)
-        evacuate(5, nc.vector.tensor_copy)
+        evacuate(5)
         turn(6)
-        evacuate(6, nc.scalar.copy)
+        evacuate(6)
         quantise(1)
         spread_bias(1)
         turn(7)
-        evacuate(7, nc.scalar.copy)
+        evacuate(7)
         for i in range(2, 7):
             quantise(i)
         turn(8)
-        evacuate(8, nc.scalar.copy)
+        evacuate(8)
         turn(9)
-        evacuate(9, nc.scalar.copy)
+        evacuate(9)
         quantise(7)
         nc.vector.tensor_scalar_min(out=clipped[:], in0=norms[:, 0:X_BLOCKS], scalar1=1.0 - 1e-7)
         turn(10)
-        evacuate(10, nc.scalar.copy)
+        evacuate(10)
         quantise(8)
         nc.vector.reciprocal(out=inv_norms[:], in_=norms[:])
         nc.vector.tensor_copy(out=b_all[:], in_=b_psum[:])
         multiply(0, 1)
         turn(11)
         square_mx(0, 1)
-        evacuate(11, nc.scalar.copy)
+        evacuate(11)
         multiply(0, 2)
         quantise(9)
         quantise(10)
@@ -249,7 +249,11 @@ def tile_directnodecomphyperbolicforecaster_pa_kernel(tc, v_init, W_vel, b_vel, 
         mxn = wide("mxn", X_BLOCKS)
 
         def norms_of_mx(c):
-            nc.vector.tensor_add(out=s[:, c], in0=mx_sq[:, 0, c], in1=mx_sq[:, 1, c])
+            for t in range(c.start, c.stop):
+                nc.scalar.activation(
+                    out=s[:, t : t + 1], in_=mx_sq[:, 1, t : t + 1], func=ACT.Identity,
+                    bias=mx_sq[:, 0, t : t + 1], scale=1.0,
+                )
             nc.gpsimd.tensor_tensor(out=mxn[:, c], in0=s[:, c], in1=half[:, c], op=ALU.pow)
 
         square_mx(0, 0)
@@ -257,12 +261,12 @@ def tile_directnodecomphyperbolicforecaster_pa_kernel(tc, v_init, W_vel, b_vel, 
         square_mx(1, 1)
         square_mx(1, 0)
         dot_mx(1, 1)
-        square_mx(1, 2)
         norms_of_mx(slice(0, 2))
+        square_mx(1, 2)
         dot_mx(1, 0)
         square_mx(1, 3)
-        dot_mx(1, 2)
         norms_of_mx(slice(2, 4))
+        dot_mx(1, 2)
         dot_mx(1, 3)
         d = wide("d", X_BLOCKS)
         nc.vector.tensor_add(out=d[:], in0=mx_b[:, 0, :], in1=mx_b[:, 1, :])
@@ -286,28 +290,20 @@ def tile_directnodecomphyperbolicforecaster_pa_kernel(tc, v_init, W_vel, b_vel, 
         )
         qq = wide("qq", 1)
         nc.vector.tensor_mul(out=qq[:], in0=b_tanh[:], in1=b_tanh[:])
-        q_scale = wide("q_scale", 1)
-        nc.vector.tensor_mul(out=q_scale[:], in0=b_tanh[:], in1=inv_bn)
-        qq_plus_1 = wide("qq_plus_1", 1)
-        nc.vector.tensor_scalar(
-            out=qq_plus_1[:], in0=b_tanh[:], scalar1=b_tanh[:, 0:1], scalar2=1.0, op0=ALU.mult, op1=ALU.add
-        )
-        t1 = wide("t1", X_BLOCKS)
-        stt(out=t1[:], in0=w[:], scalar=q_twice[:, 0:1], in1=th[:], op0=ALU.mult, op1=ALU.mult)
         p2 = wide("p2", X_BLOCKS)
         nc.vector.tensor_mul(out=p2[:], in0=th[:], in1=th[:])
-        edge_bias = wide("edge_bias", 1)
-        nc.vector.tensor_scalar(
-            out=edge_bias[:], in0=qq[:], scalar1=-0.5 / (MAXN * MAXN), scalar2=0.5 / (MAXN * MAXN),
-            op0=ALU.mult, op1=ALU.add,
-        )
+        t1 = wide("t1", X_BLOCKS)
+        stt(out=t1[:], in0=w[:], scalar=q_twice[:, 0:1], in1=th[:], op0=ALU.mult, op1=ALU.mult)
         edge_scale = wide("edge_scale", 1)
         nc.vector.tensor_scalar(
             out=edge_scale[:], in0=qq[:], scalar1=0.5 / (MAXN * MAXN), scalar2=-0.5 / (MAXN * MAXN),
             op0=ALU.mult, op1=ALU.add,
         )
-        den_1 = wide("den_1", X_BLOCKS)
-        stt(out=den_1[:], in0=p2[:], scalar=qq[:, 0:1], in1=t1[:], op0=ALU.mult, op1=ALU.add)
+        edge_bias = wide("edge_bias", 1)
+        nc.vector.tensor_scalar(
+            out=edge_bias[:], in0=qq[:], scalar1=-0.5 / (MAXN * MAXN), scalar2=0.5 / (MAXN * MAXN),
+            op0=ALU.mult, op1=ALU.add,
+        )
         edge = wide("edge", X_BLOCKS)
         nc.scalar.activation(
             out=edge[:], in_=p2[:], func=ACT.Identity, scale=edge_scale[:, 0:1], bias=edge_bias[:, 0:1]
@@ -316,8 +312,16 @@ def tile_directnodecomphyperbolicforecaster_pa_kernel(tc, v_init, W_vel, b_vel, 
         nc.scalar.activation(
             out=one_minus_p2[:], in_=p2[:], func=ACT.Identity, scale=-1.0, bias=ones_f[:, 0:1]
         )
+        den_1 = wide("den_1", X_BLOCKS)
+        stt(out=den_1[:], in0=p2[:], scalar=qq[:, 0:1], in1=t1[:], op0=ALU.mult, op1=ALU.add)
         thi = wide("thi", X_BLOCKS)
         nc.vector.tensor_mul(out=thi[:], in0=th[:], in1=inv_mxn[:])
+        qq_plus_1 = wide("qq_plus_1", 1)
+        nc.vector.tensor_scalar(
+            out=qq_plus_1[:], in0=b_tanh[:], scalar1=b_tanh[:, 0:1], scalar2=1.0, op0=ALU.mult, op1=ALU.add
+        )
+        q_scale = wide("q_scale", 1)
+        nc.vector.tensor_mul(out=q_scale[:], in0=b_tanh[:], in1=inv_bn)
         den = wide("den", X_BLOCKS)
         nc.vector.tensor_scalar(
             out=den[:], in0=den_1[:], scalar1=1.0, scalar2=EPS, op0=ALU.add, op1=ALU.max
@@ -348,8 +352,8 @@ def tile_directnodecomphyperbolicforecaster_pa_kernel(tc, v_init, W_vel, b_vel, 
                 out=b_term[t][:, cols], in_=b_all[:, cols], func=ACT.Copy, scale=coef_b[:, t : t + 1]
             )
 
-        def bias_vector(t, h):
-            cols = slice(BANK * h, BANK * (h + 1))
+        def bias_vector(t, h, cols=None):
+            cols = cols or slice(BANK * h, BANK * (h + 1))
             nc.vector.tensor_scalar_mul(
                 out=b_term[t][:, cols], in0=b_all[:, cols], scalar1=coef_b[:, t : t + 1]
             )
@@ -361,10 +365,11 @@ def tile_directnodecomphyperbolicforecaster_pa_kernel(tc, v_init, W_vel, b_vel, 
                 op0=ALU.mult, op1=ALU.add,
             )
 
-        def finish(t, h):
-            cols = slice(BANK * h, BANK * (h + 1))
+        def finish(t, h, cols=None):
+            cols = cols or slice(BANK * h, BANK * (h + 1))
             stt(
-                out=result[t][:, cols], in0=mx[(h, t)][:], scalar=coef_mx[:, t : t + 1],
+                out=result[t][:, cols], in0=mx[(h, t)][:, cols.start - BANK * h : cols.stop - BANK * h],
+                scalar=coef_mx[:, t : t + 1],
                 in1=b_term[t][:, cols], op0=ALU.mult, op1=ALU.add,
             )
 
@@ -380,30 +385,38 @@ def tile_directnodecomphyperbolicforecaster_pa_kernel(tc, v_init, W_vel, b_vel, 
             cols = slice(BANK * h, BANK * (h + 1))
             nc.gpsimd.tensor_add(out=result[t][:, cols], in0=scaled[(t, h)][:], in1=b_term[t][:, cols])
 
-        def store(t, h0, h1):
-            cols = slice(BANK * h0, BANK * h1)
+        def store(t, cols):
             nc.sync.dma_start(out=out[P * t : P * (t + 1), cols], in_=result[t][:, cols])
 
-        bias_vector(0, 0)
-        bias(0, 1)
+        quarters = [slice(BANK // 2 * j, BANK // 2 * (j + 1)) for j in range(2 * HALVES)]
+        halves = [slice(BANK * h, BANK * (h + 1)) for h in range(HALVES)]
+
         bias_gpsimd(1, 1)
         scale_scalar(1, 1)
-        bias(1, 0)
-        finish(0, 0)
+        bias_vector(0, 0, quarters[0])
+        bias_vector(0, 0, quarters[1])
+        bias_vector(0, 1)
+        finish(0, 0, quarters[0])
+        store(0, quarters[0])
+        finish(0, 0, quarters[1])
+        store(0, quarters[1])
         finish(0, 1)
-        store(0, 0, 2)
+        store(0, halves[1])
+        bias(1, 0)
         bias(2, 0)
         finish_gpsimd(1, 1)
         bias_gpsimd(3, 1)
-        scale_scalar(3, 1)
         finish(1, 0)
-        store(1, 0, 2)
+        store(1, halves[0])
+        store(1, halves[1])
+        scale_scalar(3, 1)
         bias(2, 1)
-        bias_vector(3, 0)
         finish(2, 0)
-        finish(3, 0)
-        store(3, 0, 1)
-        finish(2, 1)
-        store(2, 0, 2)
+        store(2, halves[0])
         finish_gpsimd(3, 1)
-        store(3, 1, 2)
+        bias(3, 0)
+        finish(2, 1)
+        store(2, halves[1])
+        finish(3, 0)
+        store(3, halves[0])
+        store(3, halves[1])

@@ -28,6 +28,7 @@ EPS = 1e-15
 MAXN = 1.0 - 1e-5
 EDGE = 1.5 - 0.5 / (MAXN * MAXN)
 FLOPS = 2 * ROWS * K * N
+WARM_UP = 16
 
 
 def tile_directnodecomphyperbolicforecaster_pa_kernel(tc, v_init, W_vel, b_vel, out):
@@ -49,11 +50,17 @@ def tile_directnodecomphyperbolicforecaster_pa_kernel(tc, v_init, W_vel, b_vel, 
                 source = v_init[P * i : P * (i + 1), :]
             else:
                 source = W_vel[P * (i - X_BLOCKS) : P * (i - X_BLOCKS + 1), :]
-            nc.sync.dma_start(out=rows[:], in_=source)
+            if i == 0:
+                for cols in (slice(0, K // 2), slice(K // 2, K)):
+                    nc.sync.dma_start(out=rows[:, cols], in_=source[:, cols])
+            else:
+                nc.sync.dma_start(out=rows[:], in_=source)
             blocks.append(rows)
         b_row0 = keep.tile([P, N], BF16, name="b_row0")
         first = wide("first", 1)
         nc.vector.memset(first[:], 1.0)
+        ones = keep.tile([P, P], BF16, name="ones")
+        nc.vector.memset(ones[:], 1.0)
         nc.vector.memset(b_row0[:].bitcast(I32), 0)
         nc.scalar.dma_start(out=b_row0[0:1, :], in_=b_vel.rearrange("(o n) -> o n", o=1))
 
@@ -63,10 +70,11 @@ def tile_directnodecomphyperbolicforecaster_pa_kernel(tc, v_init, W_vel, b_vel, 
         make_identity(nc, ident[:])
         half = wide("half", X_BLOCKS + 1)
         nc.gpsimd.memset(half[:], 0.5)
-        ones = keep.tile([P, P], BF16, name="ones")
-        nc.vector.memset(ones[:], 1.0)
         ones_f = wide("ones_f", P)
         nc.vector.memset(ones_f[:], 1.0)
+        idle = psum.tile([P, P], F32, tag="bank6", name="idle")
+        for turn_on in range(WARM_UP):
+            nc.tensor.matmul(idle[:], lhsT=ones[:], rhs=ones[:], start=True, stop=True)
 
         x_codes = keep.tile([P, X_BLOCKS * PASSES * P], U32, align_bytes=64, name="x_codes")
         x_scales = keep.tile([P, X_BLOCKS * PASSES * P], U8, align_bytes=64, name="x_scales")

@@ -1,4 +1,3 @@
-import math
 from contextlib import ExitStack
 
 import concourse.mybir as mybir
@@ -28,7 +27,6 @@ EPS = 1e-15
 MAXN = 1.0 - 1e-5
 EDGE = 1.5 - 0.5 / (MAXN * MAXN)
 FLOPS = 2 * ROWS * K * N
-WARM_UP = 16
 
 
 def tile_directnodecomphyperbolicforecaster_pa_kernel(tc, v_init, W_vel, b_vel, out):
@@ -59,8 +57,6 @@ def tile_directnodecomphyperbolicforecaster_pa_kernel(tc, v_init, W_vel, b_vel, 
         b_row0 = keep.tile([P, N], BF16, name="b_row0")
         first = wide("first", 1)
         nc.vector.memset(first[:], 1.0)
-        ones = keep.tile([P, P], BF16, name="ones")
-        nc.vector.memset(ones[:], 1.0)
         nc.vector.memset(b_row0[:].bitcast(I32), 0)
         nc.scalar.dma_start(out=b_row0[0:1, :], in_=b_vel.rearrange("(o n) -> o n", o=1))
 
@@ -70,11 +66,10 @@ def tile_directnodecomphyperbolicforecaster_pa_kernel(tc, v_init, W_vel, b_vel, 
         make_identity(nc, ident[:])
         half = wide("half", X_BLOCKS + 1)
         nc.gpsimd.memset(half[:], 0.5)
+        ones = keep.tile([P, P], BF16, name="ones")
+        nc.vector.memset(ones[:], 1.0)
         ones_f = wide("ones_f", P)
         nc.vector.memset(ones_f[:], 1.0)
-        idle = psum.tile([P, P], F32, tag="bank6", name="idle")
-        for turn_on in range(WARM_UP):
-            nc.tensor.matmul(idle[:], lhsT=ones[:], rhs=ones[:], start=True, stop=True)
 
         x_codes = keep.tile([P, X_BLOCKS * PASSES * P], U32, align_bytes=64, name="x_codes")
         x_scales = keep.tile([P, X_BLOCKS * PASSES * P], U8, align_bytes=64, name="x_scales")
@@ -221,10 +216,10 @@ def tile_directnodecomphyperbolicforecaster_pa_kernel(tc, v_init, W_vel, b_vel, 
         quantise(8)
         nc.vector.reciprocal(out=inv_norms[:], in_=norms[:])
         nc.vector.tensor_copy(out=b_all[:], in_=b_psum[:])
-        multiply(0, 1)
         turn(11)
-        square_mx(0, 1)
         evacuate(11)
+        multiply(0, 1)
+        square_mx(0, 1)
         multiply(0, 2)
         quantise(9)
         quantise(10)
@@ -258,9 +253,9 @@ def tile_directnodecomphyperbolicforecaster_pa_kernel(tc, v_init, W_vel, b_vel, 
 
         def norms_of_mx(c):
             for t in range(c.start, c.stop):
-                nc.scalar.activation(
-                    out=s[:, t : t + 1], in_=mx_sq[:, 1, t : t + 1], func=ACT.Identity,
-                    bias=mx_sq[:, 0, t : t + 1], scale=1.0,
+                nc.vector.tensor_scalar(
+                    out=s[:, t : t + 1], in0=mx_sq[:, 0, t : t + 1], scalar1=mx_sq[:, 1, t : t + 1],
+                    scalar2=EPS, op0=ALU.add, op1=ALU.max,
                 )
             nc.gpsimd.tensor_tensor(out=mxn[:, c], in0=s[:, c], in1=half[:, c], op=ALU.pow)
 
@@ -273,15 +268,13 @@ def tile_directnodecomphyperbolicforecaster_pa_kernel(tc, v_init, W_vel, b_vel, 
         square_mx(1, 2)
         dot_mx(1, 0)
         square_mx(1, 3)
-        norms_of_mx(slice(2, 4))
         dot_mx(1, 2)
+        norms_of_mx(slice(2, 4))
         dot_mx(1, 3)
         d = wide("d", X_BLOCKS)
         nc.vector.tensor_add(out=d[:], in0=mx_b[:, 0, :], in1=mx_b[:, 1, :])
-        mxn_c = wide("mxn_c", X_BLOCKS)
-        nc.vector.tensor_scalar_max(out=mxn_c[:], in0=mxn[:], scalar1=math.sqrt(EPS))
         inv_mxn = wide("inv_mxn", X_BLOCKS)
-        nc.vector.reciprocal(out=inv_mxn[:], in_=mxn_c[:])
+        nc.vector.reciprocal(out=inv_mxn[:], in_=mxn[:])
         w = wide("w", X_BLOCKS)
         nc.vector.tensor_mul(out=w[:], in0=d[:], in1=inv_mxn[:])
         b_tanh = wide("b_tanh", 1)
@@ -360,8 +353,8 @@ def tile_directnodecomphyperbolicforecaster_pa_kernel(tc, v_init, W_vel, b_vel, 
                 out=b_term[t][:, cols], in_=b_all[:, cols], func=ACT.Copy, scale=coef_b[:, t : t + 1]
             )
 
-        def bias_vector(t, h, cols=None):
-            cols = cols or slice(BANK * h, BANK * (h + 1))
+        def bias_vector(t, h):
+            cols = slice(BANK * h, BANK * (h + 1))
             nc.vector.tensor_scalar_mul(
                 out=b_term[t][:, cols], in0=b_all[:, cols], scalar1=coef_b[:, t : t + 1]
             )
@@ -373,11 +366,10 @@ def tile_directnodecomphyperbolicforecaster_pa_kernel(tc, v_init, W_vel, b_vel, 
                 op0=ALU.mult, op1=ALU.add,
             )
 
-        def finish(t, h, cols=None):
-            cols = cols or slice(BANK * h, BANK * (h + 1))
+        def finish(t, h):
+            cols = slice(BANK * h, BANK * (h + 1))
             stt(
-                out=result[t][:, cols], in0=mx[(h, t)][:, cols.start - BANK * h : cols.stop - BANK * h],
-                scalar=coef_mx[:, t : t + 1],
+                out=result[t][:, cols], in0=mx[(h, t)][:], scalar=coef_mx[:, t : t + 1],
                 in1=b_term[t][:, cols], op0=ALU.mult, op1=ALU.add,
             )
 
@@ -396,18 +388,14 @@ def tile_directnodecomphyperbolicforecaster_pa_kernel(tc, v_init, W_vel, b_vel, 
         def store(t, cols):
             nc.sync.dma_start(out=out[P * t : P * (t + 1), cols], in_=result[t][:, cols])
 
-        quarters = [slice(BANK // 2 * j, BANK // 2 * (j + 1)) for j in range(2 * HALVES)]
         halves = [slice(BANK * h, BANK * (h + 1)) for h in range(HALVES)]
 
         bias_gpsimd(1, 1)
         scale_scalar(1, 1)
-        bias_vector(0, 0, quarters[0])
-        bias_vector(0, 0, quarters[1])
+        bias_vector(0, 0)
         bias_vector(0, 1)
-        finish(0, 0, quarters[0])
-        store(0, quarters[0])
-        finish(0, 0, quarters[1])
-        store(0, quarters[1])
+        finish(0, 0)
+        store(0, halves[0])
         finish(0, 1)
         store(0, halves[1])
         bias(1, 0)
@@ -415,16 +403,14 @@ def tile_directnodecomphyperbolicforecaster_pa_kernel(tc, v_init, W_vel, b_vel, 
         finish_gpsimd(1, 1)
         bias_gpsimd(3, 1)
         finish(1, 0)
-        store(1, halves[0])
-        store(1, halves[1])
+        store(1, slice(0, N))
         scale_scalar(3, 1)
         bias(2, 1)
         finish(2, 0)
-        store(2, halves[0])
         finish_gpsimd(3, 1)
         bias(3, 0)
         finish(2, 1)
-        store(2, halves[1])
+        store(2, slice(0, N))
         finish(3, 0)
         store(3, halves[0])
         store(3, halves[1])

@@ -171,16 +171,20 @@ def tile_directnodecomphyperbolicforecaster_pa_kernel(tc, v_init, W_vel, b_vel, 
         evacuate(1)
         square_rows(1)
         turn(2)
-        b_tot = psum.tile([P, 1], F32, tag="bank7", name="b_tot")
-        nc.tensor.matmul(b_tot[:], lhsT=ones_f[:], rhs=b_part[:], start=True, stop=True)
-        square_rows_scalar(3)
-        nc.vector.tensor_copy(out=sums[:, X_BLOCKS : X_BLOCKS + 1], in_=b_tot[:])
-        square_rows(2)
-        turn(3)
         evacuate(2)
+        square_rows(2)
+        square_rows_scalar(3)
+        turn(3)
         evacuate(3)
+        quantise(0)
         turn(4)
         evacuate(4)
+        quantise(1)
+        quantise(2)
+        turn(5)
+        evacuate(5)
+        b_tot = psum.tile([P, 1], F32, tag="bank1", name="b_tot")
+        nc.tensor.matmul(b_tot[:], lhsT=ones_f[:], rhs=b_part[:], start=True, stop=True)
         b_psum = psum.tile([P, N], BF16, tag="bank0", name="b_psum")
 
         def spread_bias(h):
@@ -188,65 +192,57 @@ def tile_directnodecomphyperbolicforecaster_pa_kernel(tc, v_init, W_vel, b_vel, 
             nc.tensor.matmul(b_psum[:, cols], lhsT=ones[:], rhs=b_row0[:, cols], start=True, stop=True)
 
         spread_bias(0)
-        turn(5)
+        spread_bias(1)
+        nc.vector.tensor_copy(out=sums[:, X_BLOCKS : X_BLOCKS + 1], in_=b_tot[:])
         sums_c = wide("sums_c", X_BLOCKS + 1)
         norms = wide("norms", X_BLOCKS + 1)
         inv_norms = wide("inv_norms", X_BLOCKS + 1)
         clipped = wide("clipped", X_BLOCKS)
         nc.vector.tensor_scalar_max(out=sums_c[:], in0=sums[:], scalar1=EPS)
         nc.gpsimd.tensor_tensor(out=norms[:], in0=sums_c[:], in1=half[:], op=ALU.pow)
-        quantise(0)
-        evacuate(5)
+        quantise(3)
         turn(6)
         evacuate(6)
-        quantise(1)
-        spread_bias(1)
+        quantise(4)
+        quantise(5)
         turn(7)
         evacuate(7)
-        for i in range(2, 7):
-            quantise(i)
         turn(8)
         evacuate(8)
+        quantise(6)
+        quantise(7)
+        nc.vector.tensor_copy(out=b_all[:], in_=b_psum[:])
         turn(9)
         evacuate(9)
-        quantise(7)
         nc.vector.tensor_scalar_min(out=clipped[:], in0=norms[:, 0:X_BLOCKS], scalar1=1.0 - 1e-7)
+        nc.vector.reciprocal(out=inv_norms[:], in_=norms[:])
         turn(10)
         evacuate(10)
         quantise(8)
-        nc.vector.reciprocal(out=inv_norms[:], in_=norms[:])
-        nc.vector.tensor_copy(out=b_all[:], in_=b_psum[:])
         turn(11)
         evacuate(11)
         multiply(0, 1)
-        square_mx(0, 1)
-        multiply(0, 2)
+        multiply(0, 0)
         quantise(9)
         quantise(10)
-        multiply(0, 0)
+        multiply(0, 2)
         multiply(0, 3)
-        dot_mx(0, 1)
         quantise(11)
+        multiply(1, 1)
+        multiply(1, 0)
+        multiply(1, 2)
+        multiply(1, 3)
+        square_mx(0, 1)
+        dot_mx(0, 0)
+        dot_mx(0, 1)
+        square_mx(0, 2)
+        square_mx(0, 0)
+        dot_mx(0, 2)
         log_plus = wide("log_plus", X_BLOCKS)
         nc.scalar.activation(out=log_plus[:], in_=clipped[:], func=ACT.Ln, bias=ones_f[:, 0:1], scale=1.0)
         log_minus = wide("log_minus", X_BLOCKS)
         nc.scalar.activation(
             out=log_minus[:], in_=clipped[:], func=ACT.Ln, bias=ones_f[:, 0:1], scale=-1.0
-        )
-        square_mx(0, 2)
-        dot_mx(0, 0)
-        multiply(1, 1)
-        multiply(1, 0)
-        multiply(1, 2)
-        multiply(1, 3)
-        square_mx(0, 3)
-        dot_mx(0, 2)
-        twice_artanh = wide("twice_artanh", X_BLOCKS)
-        nc.vector.tensor_sub(out=twice_artanh[:], in0=log_plus[:], in1=log_minus[:])
-        gain = wide("gain", X_BLOCKS)
-        stt(
-            out=gain[:], in0=twice_artanh[:], scalar=0.5, in1=inv_norms[:, 0:X_BLOCKS], op0=ALU.mult,
-            op1=ALU.mult,
         )
         s = wide("s", X_BLOCKS)
         mxn = wide("mxn", X_BLOCKS)
@@ -259,17 +255,25 @@ def tile_directnodecomphyperbolicforecaster_pa_kernel(tc, v_init, W_vel, b_vel, 
                 )
             nc.gpsimd.tensor_tensor(out=mxn[:, c], in0=s[:, c], in1=half[:, c], op=ALU.pow)
 
-        square_mx(0, 0)
+        square_mx(0, 3)
+        twice_artanh = wide("twice_artanh", X_BLOCKS)
+        nc.vector.tensor_sub(out=twice_artanh[:], in0=log_plus[:], in1=log_minus[:])
+        gain = wide("gain", X_BLOCKS)
+        stt(
+            out=gain[:], in0=twice_artanh[:], scalar=0.5, in1=inv_norms[:, 0:X_BLOCKS], op0=ALU.mult,
+            op1=ALU.mult,
+        )
         dot_mx(0, 3)
         square_mx(1, 1)
         square_mx(1, 0)
         dot_mx(1, 1)
         norms_of_mx(slice(0, 2))
-        square_mx(1, 2)
         dot_mx(1, 0)
+        square_mx(1, 2)
+        norms_of_mx(slice(2, 3))
         square_mx(1, 3)
         dot_mx(1, 2)
-        norms_of_mx(slice(2, 4))
+        norms_of_mx(slice(3, 4))
         dot_mx(1, 3)
         d = wide("d", X_BLOCKS)
         nc.vector.tensor_add(out=d[:], in0=mx_b[:, 0, :], in1=mx_b[:, 1, :])

from contextlib import ExitStack

import concourse.mybir as mybir
from concourse.masks import make_identity

F32 = mybir.dt.float32
BF16 = mybir.dt.bfloat16
U32 = mybir.dt.uint32
U8 = mybir.dt.uint8
I32 = mybir.dt.int32
FP8X4 = mybir.dt.float8_e4m3fn_x4
ALU = mybir.AluOpType
ACT = mybir.ActivationFunctionType

P = 128
ROWS = 512
K = 1024
N = 1024
PASSES = K // (4 * P)
X_BLOCKS = ROWS // P
W_BLOCKS = N // P
BANK = 512
HALVES = N // BANK
BLOCKS_PER_HALF = W_BLOCKS // HALVES

EPS = 1e-15
MAXN = 1.0 - 1e-5
EDGE = 1.5 - 0.5 / (MAXN * MAXN)
FLOPS = 2 * ROWS * K * N


def tile_directnodecomphyperbolicforecaster_pa_kernel(tc, v_init, W_vel, b_vel, out):
    nc = tc.nc
    with ExitStack() as ctx:
        ctx.enter_context(tc.manual_schedule())
        keep = ctx.enter_context(tc.tile_pool(name="keep", bufs=1))
        psum = ctx.enter_context(tc.psum_pool(name="psum", bufs=1))

        def wide(name, width):
            return keep.tile([P, width], F32, name=name)

        b_cols = keep.tile([P, N // P], BF16, name="b_cols")
        nc.scalar.dma_start(out=b_cols[:], in_=b_vel.rearrange("(p j) -> p j", p=P))
        blocks = []
        for i in range(X_BLOCKS + W_BLOCKS):
            rows = keep.tile([P, K], BF16, name="rows%d" % i)
            if i < X_BLOCKS:
                source = v_init[P * i : P * (i + 1), :]
            else:
                source = W_vel[P * (i - X_BLOCKS) : P * (i - X_BLOCKS + 1), :]
            if i == 0:
                for cols in (slice(0, K // 2), slice(K // 2, K)):
                    nc.sync.dma_start(out=rows[:, cols], in_=source[:, cols])
            else:
                nc.sync.dma_start(out=rows[:], in_=source)
            blocks.append(rows)
        b_row0 = keep.tile([P, N], BF16, name="b_row0")
        first = wide("first", 1)
        nc.vector.memset(first[:], 1.0)
        nc.vector.memset(b_row0[:].bitcast(I32), 0)
        nc.scalar.dma_start(out=b_row0[0:1, :], in_=b_vel.rearrange("(o n) -> o n", o=1))

        log_table = wide("log_table", 1)
        nc.scalar.activation(out=log_table[:], in_=first[:], func=ACT.Ln)
        ident = wide("ident", P)
        make_identity(nc, ident[:])
        half = wide("half", X_BLOCKS + 1)
        nc.gpsimd.memset(half[:], 0.5)
        ones = keep.tile([P, P], BF16, name="ones")
        nc.vector.memset(ones[:], 1.0)
        ones_f = wide("ones_f", P)
        nc.vector.memset(ones_f[:], 1.0)

        x_codes = keep.tile([P, X_BLOCKS * PASSES * P], U32, align_bytes=64, name="x_codes")
        x_scales = keep.tile([P, X_BLOCKS * PASSES * P], U8, align_bytes=64, name="x_scales")
        w_codes = keep.tile([P, PASSES, N], U32, align_bytes=64, name="w_codes")
        w_scales = keep.tile([P, PASSES, N], U8, align_bytes=64, name="w_scales")
        sums = wide("sums", X_BLOCKS + 1)
        flipped = {}
        grouped = {}

        def turn(i):
            words = blocks[i][:].bitcast(F32)
            bank = i if i < 8 else i - 4
            f = psum.tile([P, PASSES, 2, P], F32, tag="bank%d" % bank, name="flipped")
            for g in range(PASSES):
                for u in range(2):
                    start = P * (2 * g + u)
                    nc.tensor.transpose(f[:, g, u, :], words[:, start : start + P], ident[:])
            flipped[i] = f

        def evacuate(i):
            t = keep.tile([P, PASSES * 4 * P], BF16, align_bytes=64, name="grouped%d" % i)
            nc.scalar.copy(
                out=t[:].bitcast(F32).rearrange("p (g c u) -> p g c u", g=PASSES, u=2),
                in_=flipped[i][:].rearrange("p g u c -> p g c u"),
            )
            grouped[i] = t

        def quantise(i):
            if i < X_BLOCKS:
                cols = slice(PASSES * P * i, PASSES * P * (i + 1))
                nc.vector.quantize_mx(
                    out=x_codes[:, cols].bitcast(FP8X4), scales=x_scales[:, cols], in_=grouped[i][:]
                )
            else:
                cols = slice(P * (i - X_BLOCKS), P * (i - X_BLOCKS + 1))
                for g in range(PASSES):
                    nc.vector.quantize_mx(
                        out=w_codes[:, g, cols].bitcast(FP8X4), scales=w_scales[:, g, cols],
                        in_=grouped[i][:, 4 * P * g : 4 * P * (g + 1)],
                    )

        def square_rows(i):
            sq = keep.tile([P, K], BF16, name="x_sq%d" % i)
            nc.vector.scalar_tensor_tensor(
                out=sq[:], in0=blocks[i][:], scalar=1.0, in1=blocks[i][:], op0=ALU.mult,
                op1=ALU.mult, accum_out=sums[:, i : i + 1],
            )

        def square_rows_scalar(i):
            sq = keep.tile([P, K], BF16, name="x_sq%d" % i)
            nc.scalar.activation(
                out=sq[:], in_=blocks[i][:], func=ACT.Square, accum_out=sums[:, i : i + 1]
            )

        mx = {}
        mx_sq = keep.tile([P, HALVES, X_BLOCKS], F32, name="mx_sq")
        mx_b = keep.tile([P, HALVES, X_BLOCKS], F32, name="mx_b")

        def multiply(h, t):
            acc = psum.tile([P, BANK], F32, tag="bank%d" % (X_BLOCKS * h + t), name="acc")
            for g in range(PASSES):
                x_cols = slice(P * (PASSES * t + g), P * (PASSES * t + g + 1))
                n_cols = slice(BANK * h, BANK * (h + 1))
                nc.tensor.matmul_mx(
                    out=acc[:],
                    lhsT=x_codes[:, x_cols].bitcast(FP8X4), lhsT_scale=x_scales[:, x_cols],
                    rhs=w_codes[:, g, n_cols].bitcast(FP8X4), rhs_scale=w_scales[:, g, n_cols],
                    start=(g == 0), stop=(g == PASSES - 1),
                )
            mx[(h, t)] = acc

        def square_mx(h, t):
            junk = keep.tile([P, BANK], BF16, name="junk_s%d%d" % (h, t))
            nc.scalar.activation(
                out=junk[:], in_=mx[(h, t)][:], func=ACT.Square, accum_out=mx_sq[:, h, t : t + 1]
            )

        b_all = keep.tile([P, N], BF16, name="b_all")

        def dot_mx(h, t):
            junk = keep.tile([P, BANK], BF16, name="junk_d%d%d" % (h, t))
            nc.vector.scalar_tensor_tensor(
                out=junk[:], in0=mx[(h, t)][:], scalar=1.0, in1=b_all[:, BANK * h : BANK * (h + 1)],
                op0=ALU.mult, op1=ALU.mult, accum_out=mx_b[:, h, t : t + 1],
            )

        stt = nc.vector.scalar_tensor_tensor

        b_sq = wide("b_sq", N // P)
        b_part = wide("b_part", 1)
        stt(
            out=b_sq[:], in0=b_cols[:], scalar=1.0, in1=b_cols[:], op0=ALU.mult, op1=ALU.mult,
            accum_out=b_part[:],
        )
        turn(0)
        evacuate(0)
        square_rows(0)
        turn(1)
        evacuate(1)
        square_rows(1)
        turn(2)
        evacuate(2)
        square_rows(2)
        square_rows_scalar(3)
        turn(3)
        evacuate(3)
        quantise(0)
        turn(4)
        evacuate(4)
        quantise(1)
        quantise(2)
        turn(5)
        evacuate(5)
        b_tot = psum.tile([P, 1], F32, tag="bank1", name="b_tot")
        nc.tensor.matmul(b_tot[:], lhsT=ones_f[:], rhs=b_part[:], start=True, stop=True)
        b_psum = psum.tile([P, N], BF16, tag="bank0", name="b_psum")

        def spread_bias(h):
            cols = slice(BANK * h, BANK * (h + 1))
            nc.tensor.matmul(b_psum[:, cols], lhsT=ones[:], rhs=b_row0[:, cols], start=True, stop=True)

        spread_bias(0)
        spread_bias(1)
        nc.vector.tensor_copy(out=sums[:, X_BLOCKS : X_BLOCKS + 1], in_=b_tot[:])
        sums_c = wide("sums_c", X_BLOCKS + 1)
        norms = wide("norms", X_BLOCKS + 1)
        inv_norms = wide("inv_norms", X_BLOCKS + 1)
        clipped = wide("clipped", X_BLOCKS)
        nc.vector.tensor_scalar_max(out=sums_c[:], in0=sums[:], scalar1=EPS)
        nc.gpsimd.tensor_tensor(out=norms[:], in0=sums_c[:], in1=half[:], op=ALU.pow)
        quantise(3)
        turn(6)
        evacuate(6)
        quantise(4)
        quantise(5)
        turn(7)
        evacuate(7)
        turn(8)
        evacuate(8)
        quantise(6)
        quantise(7)
        nc.vector.tensor_copy(out=b_all[:], in_=b_psum[:])
        turn(9)
        evacuate(9)
        nc.vector.tensor_scalar_min(out=clipped[:], in0=norms[:, 0:X_BLOCKS], scalar1=1.0 - 1e-7)
        nc.vector.reciprocal(out=inv_norms[:], in_=norms[:])
        turn(10)
        evacuate(10)
        quantise(8)
        turn(11)
        evacuate(11)
        multiply(0, 1)
        multiply(0, 0)
        quantise(9)
        quantise(10)
        multiply(0, 2)
        multiply(0, 3)
        quantise(11)
        multiply(1, 1)
        multiply(1, 0)
        multiply(1, 2)
        multiply(1, 3)
        square_mx(0, 1)
        dot_mx(0, 0)
        dot_mx(0, 1)
        square_mx(0, 2)
        square_mx(0, 0)
        dot_mx(0, 2)
        log_plus = wide("log_plus", X_BLOCKS)
        nc.scalar.activation(out=log_plus[:], in_=clipped[:], func=ACT.Ln, bias=ones_f[:, 0:1], scale=1.0)
        log_minus = wide("log_minus", X_BLOCKS)
        nc.scalar.activation(
            out=log_minus[:], in_=clipped[:], func=ACT.Ln, bias=ones_f[:, 0:1], scale=-1.0
        )
        s = wide("s", X_BLOCKS)
        mxn = wide("mxn", X_BLOCKS)

        def norms_of_mx(c):
            for t in range(c.start, c.stop):
                nc.vector.tensor_scalar(
                    out=s[:, t : t + 1], in0=mx_sq[:, 0, t : t + 1], scalar1=mx_sq[:, 1, t : t + 1],
                    scalar2=EPS, op0=ALU.add, op1=ALU.max,
                )
            nc.gpsimd.tensor_tensor(out=mxn[:, c], in0=s[:, c], in1=half[:, c], op=ALU.pow)

        square_mx(0, 3)
        twice_artanh = wide("twice_artanh", X_BLOCKS)
        nc.vector.tensor_sub(out=twice_artanh[:], in0=log_plus[:], in1=log_minus[:])
        gain = wide("gain", X_BLOCKS)
        stt(
            out=gain[:], in0=twice_artanh[:], scalar=0.5, in1=inv_norms[:, 0:X_BLOCKS], op0=ALU.mult,
            op1=ALU.mult,
        )
        dot_mx(0, 3)
        square_mx(1, 1)
        square_mx(1, 0)
        dot_mx(1, 1)
        norms_of_mx(slice(0, 2))
        dot_mx(1, 0)
        square_mx(1, 2)
        norms_of_mx(slice(2, 3))
        square_mx(1, 3)
        dot_mx(1, 2)
        norms_of_mx(slice(3, 4))
        dot_mx(1, 3)
        d = wide("d", X_BLOCKS)
        nc.vector.tensor_add(out=d[:], in0=mx_b[:, 0, :], in1=mx_b[:, 1, :])
        inv_mxn = wide("inv_mxn", X_BLOCKS)
        nc.vector.reciprocal(out=inv_mxn[:], in_=mxn[:])
        w = wide("w", X_BLOCKS)
        nc.vector.tensor_mul(out=w[:], in0=d[:], in1=inv_mxn[:])
        b_tanh = wide("b_tanh", 1)
        nc.scalar.activation(out=b_tanh[:], in_=norms[:, X_BLOCKS : X_BLOCKS + 1], func=ACT.Tanh)
        th = wide("th", X_BLOCKS)
        for t in range(X_BLOCKS):
            nc.scalar.activation(
                out=th[:, t : t + 1], in_=mxn[:, t : t + 1], func=ACT.Tanh, scale=gain[:, t : t + 1]
            )
        inv_bn = inv_norms[:, X_BLOCKS : X_BLOCKS + 1]
        q_twice = wide("q_twice", 1)
        nc.vector.tensor_scalar(
            out=q_twice[:], in0=b_tanh[:], scalar1=inv_bn, scalar2=2.0, op0=ALU.mult, op1=ALU.mult
        )
        qq = wide("qq", 1)
        nc.vector.tensor_mul(out=qq[:], in0=b_tanh[:], in1=b_tanh[:])
        p2 = wide("p2", X_BLOCKS)
        nc.vector.tensor_mul(out=p2[:], in0=th[:], in1=th[:])
        t1 = wide("t1", X_BLOCKS)
        stt(out=t1[:], in0=w[:], scalar=q_twice[:, 0:1], in1=th[:], op0=ALU.mult, op1=ALU.mult)
        edge_scale = wide("edge_scale", 1)
        nc.vector.tensor_scalar(
            out=edge_scale[:], in0=qq[:], scalar1=0.5 / (MAXN * MAXN), scalar2=-0.5 / (MAXN * MAXN),
            op0=ALU.mult, op1=ALU.add,
        )
        edge_bias = wide("edge_bias", 1)
        nc.vector.tensor_scalar(
            out=edge_bias[:], in0=qq[:], scalar1=-0.5 / (MAXN * MAXN), scalar2=0.5 / (MAXN * MAXN),
            op0=ALU.mult, op1=ALU.add,
        )
        edge = wide("edge", X_BLOCKS)
        nc.scalar.activation(
            out=edge[:], in_=p2[:], func=ACT.Identity, scale=edge_scale[:, 0:1], bias=edge_bias[:, 0:1]
        )
        one_minus_p2 = wide("one_minus_p2", X_BLOCKS)
        nc.scalar.activation(
            out=one_minus_p2[:], in_=p2[:], func=ACT.Identity, scale=-1.0, bias=ones_f[:, 0:1]
        )
        den_1 = wide("den_1", X_BLOCKS)
        stt(out=den_1[:], in0=p2[:], scalar=qq[:, 0:1], in1=t1[:], op0=ALU.mult, op1=ALU.add)
        thi = wide("thi", X_BLOCKS)
        nc.vector.tensor_mul(out=thi[:], in0=th[:], in1=inv_mxn[:])
        qq_plus_1 = wide("qq_plus_1", 1)
        nc.vector.tensor_scalar(
            out=qq_plus_1[:], in0=b_tanh[:], scalar1=b_tanh[:, 0:1], scalar2=1.0, op0=ALU.mult, op1=ALU.add
        )
        q_scale = wide("q_scale", 1)
        nc.vector.tensor_mul(out=q_scale[:], in0=b_tanh[:], in1=inv_bn)
        den = wide("den", X_BLOCKS)
        nc.vector.tensor_scalar(
            out=den[:], in0=den_1[:], scalar1=1.0, scalar2=EPS, op0=ALU.add, op1=ALU.max
        )
        ar = wide("ar", X_BLOCKS)
        stt(out=ar[:], in0=t1[:], scalar=qq_plus_1[:, 0:1], in1=thi[:], op0=ALU.add, op1=ALU.mult)
        inv = wide("inv", X_BLOCKS)
        nc.vector.reciprocal(out=inv[:], in_=den[:])
        shrink_den = wide("shrink_den", X_BLOCKS)
        stt(out=shrink_den[:], in0=den[:], scalar=EDGE, in1=edge[:], op0=ALU.mult, op1=ALU.add)
        shrink = wide("shrink", X_BLOCKS)
        nc.vector.tensor_mul(out=shrink[:], in0=shrink_den[:], in1=inv[:])
        cbi = wide("cbi", X_BLOCKS)
        stt(out=cbi[:], in0=one_minus_p2[:], scalar=q_scale[:, 0:1], in1=inv[:], op0=ALU.mult, op1=ALU.mult)
        ari = wide("ari", X_BLOCKS)
        nc.vector.tensor_mul(out=ari[:], in0=ar[:], in1=inv[:])
        coef_b = wide("coef_b", X_BLOCKS)
        stt(out=coef_b[:], in0=shrink[:], scalar=1.0, in1=cbi[:], op0=ALU.min, op1=ALU.mult)
        coef_mx = wide("coef_mx", X_BLOCKS)
        stt(out=coef_mx[:], in0=shrink[:], scalar=1.0, in1=ari[:], op0=ALU.min, op1=ALU.mult)

        b_term = [wide("b_term%d" % t, N) for t in range(X_BLOCKS)]
        result = [wide("result%d" % t, N) for t in range(X_BLOCKS)]

        def bias(t, h):
            cols = slice(BANK * h, BANK * (h + 1))
            nc.scalar.activation(
                out=b_term[t][:, cols], in_=b_all[:, cols], func=ACT.Copy, scale=coef_b[:, t : t + 1]
            )

        def bias_vector(t, h):
            cols = slice(BANK * h, BANK * (h + 1))
            nc.vector.tensor_scalar_mul(
                out=b_term[t][:, cols], in0=b_all[:, cols], scalar1=coef_b[:, t : t + 1]
            )

        def bias_gpsimd(t, h):
            cols = slice(BANK * h, BANK * (h + 1))
            nc.gpsimd.tensor_scalar(
                out=b_term[t][:, cols], in0=b_all[:, cols], scalar1=coef_b[:, t : t + 1], scalar2=0.0,
                op0=ALU.mult, op1=ALU.add,
            )

        def finish(t, h):
            cols = slice(BANK * h, BANK * (h + 1))
            stt(
                out=result[t][:, cols], in0=mx[(h, t)][:], scalar=coef_mx[:, t : t + 1],
                in1=b_term[t][:, cols], op0=ALU.mult, op1=ALU.add,
            )

        scaled = {}

        def scale_scalar(t, h):
            scaled[(t, h)] = wide("scaled%d%d" % (t, h), BANK)
            nc.scalar.activation(
                out=scaled[(t, h)][:], in_=mx[(h, t)][:], func=ACT.Copy, scale=coef_mx[:, t : t + 1]
            )

        def finish_gpsimd(t, h):
            cols = slice(BANK * h, BANK * (h + 1))
            nc.gpsimd.tensor_add(out=result[t][:, cols], in0=scaled[(t, h)][:], in1=b_term[t][:, cols])

        def store(t, cols):
            nc.sync.dma_start(out=out[P * t : P * (t + 1), cols], in_=result[t][:, cols])

        halves = [slice(BANK * h, BANK * (h + 1)) for h in range(HALVES)]

        bias_gpsimd(1, 1)
        scale_scalar(1, 1)
        bias_vector(0, 0)
        bias_vector(0, 1)
        finish(0, 0)
        store(0, halves[0])
        finish(0, 1)
        store(0, halves[1])
        bias(1, 0)
        bias(2, 0)
        finish_gpsimd(1, 1)
        bias_gpsimd(3, 1)
        finish(1, 0)
        store(1, slice(0, N))
        scale_scalar(3, 1)
        bias(2, 1)
        finish(2, 0)
        finish_gpsimd(3, 1)
        bias(3, 0)
        finish(2, 1)
        store(2, slice(0, N))
        finish(3, 0)
        store(3, halves[0])
        store(3, halves[1])
